import numpy as np
import ml_dtypes


def mxq(x, axis, fmt="e4m3"):
    dtype, down = {"e4m3": (ml_dtypes.float8_e4m3fn, 7), "e5m2": (ml_dtypes.float8_e5m2, 14)}[fmt]
    v = np.moveaxis(np.asarray(x, np.float32).astype(ml_dtypes.bfloat16).astype(np.float64), axis, -1)
    blocks = v.reshape(v.shape[:-1] + (-1, 32))
    amax = np.abs(blocks).max(-1, keepdims=True)
    byte = np.maximum(np.where(amax > 0, np.frexp(amax)[1] - 1 + 127, 0) - down, 1)
    scale = np.exp2(byte - 127.0)
    codes = (blocks / scale).astype(np.float32).astype(dtype).astype(np.float64)
    return np.moveaxis((codes * scale).reshape(v.shape), -1, axis)


WIDE = False


def mx_kscale(k):
    if not WIDE:
        return np.ones(k)
    levels = np.array([10, -10, 5, -5, 0])
    a = np.random.permutation(np.resize(levels, k // 512 * 4)).reshape(k // 512, 4)
    idx = np.arange(k)
    return np.exp2(a[idx // 512, idx % 128 // 32])


BF16 = ml_dtypes.bfloat16


def bf(x):
    return np.asarray(x, np.float32).astype(BF16)


def f64(x):
    return np.asarray(x).astype(np.float64)


B, CX, CT, N, T, C, K = 2, 256, 256, 4, 512, 512, 4
CIN = CX + CT
DH = C // K
SMALL_VALUE = -32767.0


def heads(t):
    return t.reshape(B, K, DH, N, T).transpose(1, 0, 3, 4, 2)


def setup_inputs():
    s = mx_kscale(CIN)
    return {"x": bf(np.random.standard_normal((B, CX, N, T)) * s[:CX][None, :, None, None]),
            "tem_embedding": bf(np.random.standard_normal((B, CT, N, T)) * s[CX:][None, :, None, None]),
            "Wv": bf(np.random.standard_normal((C, CIN)) / np.sqrt(CIN) / s[None, :]),
            "bv": bf(np.random.standard_normal(C) * 0.1),
            "q": bf(np.random.standard_normal((B, C, N, T)) * 1.5),
            "k": bf(np.random.standard_normal((B, C, N, T)) * 1.5)}


def reference(x, tem_embedding, Wv, bv, q, k):
    xin = np.concatenate([f64(x), f64(tem_embedding)[:, :, :, -T:]], axis=1).reshape(B, CIN, N * T)
    v = ((mxq(f64(Wv), 1, "e4m3") @ mxq(xin, 1, "e4m3")) + f64(bv)[None, :, None]).reshape(B, C, N, T)
    qh, kh, vh = heads(f64(q)), heads(f64(k)), heads(v)
    scores = qh @ kh.transpose(0, 1, 2, 4, 3) / np.sqrt(DH)
    causal = np.tril(np.ones((T, T), dtype=bool))
    scores = np.where(causal, scores, SMALL_VALUE)
    e = np.exp(scores - scores.max(-1, keepdims=True))
    out = (mxq(e, 4, "e4m3") @ mxq(vh, 3, "e4m3")) / e.sum(-1, keepdims=True)
    return out.transpose(1, 0, 4, 2, 3).reshape(B, C, N, T)

@@ -1,0 +1,308 @@
+from contextlib import ExitStack
+import math
+
+import concourse.mybir as mybir
+from concourse.masks import make_identity
+
+F32 = mybir.dt.float32
+BF16 = mybir.dt.bfloat16
+U32 = mybir.dt.uint32
+U8 = mybir.dt.uint8
+FP8X4 = mybir.dt.float8_e4m3fn_x4
+ALU = mybir.AluOpType
+ACT = mybir.ActivationFunctionType
+AXIS = mybir.AxisListType
+
+P = 128
+PACK = 4
+BATCH, NODES, HEADS, T, DH = 2, 4, 4, 512, 128
+CIN = 512
+TILES = T // P
+HALF = T // 2
+UNITS = BATCH * NODES * HEADS
+SCALE = 1.0 / math.sqrt(DH)
+MASKED = -(2.0**30)
+
+FLOPS = 3 * 2 * BATCH * NODES * T * CIN * CIN
+
+
+def tile_tatt_pa_t_kernel(tc, x, tem_embedding, Wv, bv, q, k, out):
+    nc = tc.nc
+    with ExitStack() as ctx:
+        const = ctx.enter_context(tc.tile_pool(name="const", bufs=1))
+        loads = ctx.enter_context(tc.tile_pool(name="loads", bufs=BATCH * NODES))
+        work = ctx.enter_context(tc.tile_pool(name="work", bufs=2))
+        small = ctx.enter_context(tc.tile_pool(name="small", bufs=4))
+        psum = ctx.enter_context(tc.psum_pool(name="psum", bufs=1))
+
+        q_sb, k_sb, x_sb = [], [], []
+        wv_sb = const.tile([P, PACK, CIN], BF16, name="wv_sb")
+        bias_bf = const.tile([P, CIN], BF16, name="bias_bf")
+        for group in range(BATCH * NODES):
+            b, n = divmod(group, NODES)
+            q_g = loads.tile([P, HEADS, T], BF16, name="q_g")
+            k_g = loads.tile([P, HEADS, T], BF16, name="k_g")
+            x_g = loads.tile([P, PACK, T], BF16, name="x_g")
+            nc.sync.dma_start(out=q_g[:], in_=q[b, :, n, :].rearrange("(h c) t -> c h t", c=P))
+            nc.sync.dma_start(out=k_g[:], in_=k[b, :, n, :].rearrange("(h c) t -> c h t", c=P))
+            if group == 0:
+                nc.sync.dma_start(out=wv_sb[:], in_=Wv.rearrange("(a o) c -> o a c", o=P))
+            nc.sync.dma_start(
+                out=x_g[:, 0:2, :], in_=x[b, :, n, :].rearrange("(j p) t -> p j t", p=P)
+            )
+            nc.sync.dma_start(
+                out=x_g[:, 2:4, :],
+                in_=tem_embedding[b, :, n, :].rearrange("(j p) t -> p j t", p=P),
+            )
+            if group == 0:
+                nc.sync.dma_start(out=bias_bf[:], in_=bv.partition_broadcast(P))
+            q_sb.append(q_g)
+            k_sb.append(k_g)
+            x_sb.append(x_g)
+
+        ident_bf = const.tile([P, P], BF16, name="ident_bf")
+        make_identity(nc, ident_bf[:])
+        ident_f32 = const.tile([P, P], F32, name="ident_f32")
+        make_identity(nc, ident_f32[:])
+        mask_f32 = const.tile([P, P], F32, name="mask_f32")
+        nc.gpsimd.memset(mask_f32[:], 0.0)
+        nc.gpsimd.affine_select(
+            out=mask_f32[:],
+            in_=mask_f32[:],
+            compare_op=ALU.is_ge,
+            fill=MASKED,
+            base=0,
+            pattern=[[-1, P]],
+            channel_multiplier=1,
+        )
+        mask_bf = const.tile([P, P], BF16, name="mask_bf")
+        nc.vector.tensor_copy(out=mask_bf[:], in_=mask_f32[:])
+        e_ring = []
+        for r in range(2):
+            e_r = const.tile([P, TILES * T], BF16, name="e_ring%d" % r)
+            nc.gpsimd.memset(e_r[:], 0.0)
+            e_ring.append(e_r)
+
+        live = {}
+
+        def unit_of(u):
+            group, h = divmod(u, HEADS)
+            b, n = divmod(group, NODES)
+            return group, b, n, h
+
+        def score_region(u, i):
+            if i == 3:
+                return live[("s3", u)][:, :]
+            if i == 2:
+                return live[("s20", u)][:, 0 : 3 * P]
+            if i == 0:
+                return live[("s20", u)][:, 3 * P : 4 * P]
+            return live[("s1", u)][:, :]
+
+        def scores(u, i):
+            group, b, n, h = unit_of(u)
+            region = score_region(u, i)
+            q_i = q_sb[group][:, h, i * P : (i + 1) * P]
+            diagonal = region[:, i * P : (i + 1) * P]
+            nc.tensor.matmul(diagonal, lhsT=ident_bf[:], rhs=mask_bf[:], start=True, stop=False)
+            nc.tensor.matmul(
+                diagonal, lhsT=q_i, rhs=k_sb[group][:, h, i * P : (i + 1) * P], start=False, stop=True
+            )
+            if i > 0:
+                nc.tensor.matmul(
+                    region[:, 0 : i * P], lhsT=q_i, rhs=k_sb[group][:, h, 0 : i * P], start=True, stop=True
+                )
+
+        def row_max(u, i):
+            nc.vector.tensor_reduce(
+                out=live[("max", u)][:, i : i + 1], in_=score_region(u, i), axis=AXIS.X, op=ALU.max
+            )
+
+        def exp_tile(u, i):
+            nc.scalar.activation(
+                out=e_ring[u % 2][:, i * T : i * T + (i + 1) * P],
+                in_=score_region(u, i),
+                func=ACT.Exp,
+                bias=live[("shift", u)][:, i : i + 1],
+                scale=SCALE,
+                accum_out=live[("sum", u)][:, i : i + 1],
+            )
+
+        def transpose_e(u, half):
+            e_words = e_ring[u % 2][:].bitcast(F32)
+            eT_ps = psum.tile([P, 2, HALF], F32, name="eT_ps", tag="eT", bufs=2)
+            for g in range(2):
+                for ii in range(2):
+                    i = 2 * half + ii
+                    nc.tensor.transpose(
+                        eT_ps[:, g, ii * P : (ii + 1) * P],
+                        e_words[:, i * HALF + g * P : i * HALF + (g + 1) * P],
+                        ident_f32[:],
+                    )
+            live[("eT", u, half)] = eT_ps
+
+        def regroup_e(u, half):
+            if half == 0:
+                e_grouped = work.tile([P, T * PACK], BF16, name="e_grouped", align_bytes=64)
+                live[("eg", u)] = e_grouped
+            words = live[("eg", u)][:].bitcast(F32)[:, half * T : (half + 1) * T]
+            nc.scalar.copy(
+                out=words.rearrange("p (t g) -> p t g", g=2),
+                in_=live[("eT", u, half)][:].rearrange("p g t -> p t g"),
+            )
+
+        def quantise_e(u):
+            e_codes = work.tile([P, T], U32, name="e_codes", align_bytes=64)
+            e_scales = work.tile([P, T], U8, name="e_scales", align_bytes=64)
+            nc.vector.quantize_mx(
+                out=e_codes[:].bitcast(FP8X4), scales=e_scales[:], in_=live[("eg", u)][:]
+            )
+            live[("ec", u)] = (e_codes, e_scales)
+
+        def quantise_group(group):
+            x_grouped = work.tile([P, T * PACK], BF16, name="x_grouped", align_bytes=64)
+            src = x_sb[group][:].rearrange("p j (g w r) -> p g r w j", g=2, w=P, r=2)
+            dst = x_grouped[:].rearrange("p (g r w j) -> p g r w j", g=2, r=2, w=P, j=PACK)
+            for g in range(2):
+                nc.vector.tensor_copy(out=dst[:, g], in_=src[:, g])
+            x_codes = work.tile([P, T], U32, name="x_codes", align_bytes=64)
+            x_scales = work.tile([P, T], U8, name="x_scales", align_bytes=64)
+            nc.vector.quantize_mx(out=x_codes[:].bitcast(FP8X4), scales=x_scales[:], in_=x_grouped[:])
+            live[("xc", group)] = (x_codes, x_scales)
+
+        def project_v(u):
+            group, b, n, h = unit_of(u)
+            x_codes, x_scales = live[("xc", group)]
+            v_ps = psum.tile([P, PACK, DH], F32, name="v_ps", tag="v")
+            for s in range(PACK):
+                nc.tensor.matmul_mx(
+                    out=v_ps[:, s, :],
+                    lhsT=x_codes[:, s * P : (s + 1) * P].bitcast(FP8X4),
+                    lhsT_scale=x_scales[:, s * P : (s + 1) * P],
+                    rhs=w_codes[:, h * DH : (h + 1) * DH].bitcast(FP8X4),
+                    rhs_scale=w_scales[:, h * DH : (h + 1) * DH],
+                    start=True,
+                    stop=True,
+                )
+            v_grouped = work.tile([P, DH * PACK], BF16, name="v_grouped", align_bytes=64)
+            nc.vector.tensor_tensor(
+                out=v_grouped[:].rearrange("p (c s) -> p c s", s=PACK),
+                in0=v_ps[:].rearrange("p s c -> p c s"),
+                in1=bias_f32[:, h * DH : (h + 1) * DH].unsqueeze(2).to_broadcast([P, DH, PACK]),
+                op=ALU.add,
+            )
+            v_codes = work.tile([P, DH], U32, name="v_codes", align_bytes=64, bufs=3)
+            v_scales = work.tile([P, DH], U8, name="v_scales", align_bytes=64, bufs=3)
+            nc.vector.quantize_mx(out=v_codes[:].bitcast(FP8X4), scales=v_scales[:], in_=v_grouped[:])
+            live[("vc", u)] = (v_codes, v_scales)
+
+        def attend(u):
+            e_codes, e_scales = live[("ec", u)]
+            v_codes, v_scales = live[("vc", u)]
+            oT_ps = psum.tile([P, TILES, DH], F32, name="oT_ps", tag="oT")
+            for i in range(TILES):
+                nc.tensor.matmul_mx(
+                    out=oT_ps[:, i, :],
+                    lhsT=e_codes[:, i * P : (i + 1) * P].bitcast(FP8X4),
+                    lhsT_scale=e_scales[:, i * P : (i + 1) * P],
+                    rhs=v_codes[:].bitcast(FP8X4),
+                    rhs_scale=v_scales[:],
+                    start=True,
+                    stop=True,
+                )
+            live[("oT", u)] = oT_ps
+
+        def normalise(u):
+            o_rows = work.tile([P, TILES, DH], F32, name="o_rows")
+            nc.vector.tensor_tensor(
+                out=o_rows[:],
+                in0=live[("oT", u)][:],
+                in1=live[("inv", u)][:].unsqueeze(2).to_broadcast([P, TILES, DH]),
+                op=ALU.mult,
+            )
+            live[("or", u)] = o_rows
+
+        def transpose_out(u):
+            o_rows = live[("or", u)]
+            o_ps = psum.tile([P, T], F32, name="o_ps", tag="o")
+            for i in range(TILES):
+                nc.tensor.transpose(o_ps[:, i * P : (i + 1) * P], o_rows[:, i, :], ident_f32[:])
+            live[("o", u)] = o_ps
+
+        def store(u):
+            group, b, n, h = unit_of(u)
+            o_sb = work.tile([P, T], F32, name="o_sb", bufs=4)
+            nc.scalar.copy(out=o_sb[:], in_=live[("o", u)][:])
+            nc.sync.dma_start(out=out[b, h * DH : (h + 1) * DH, n, :], in_=o_sb[:])
+
+        def open_unit(u):
+            live[("max", u)] = small.tile([P, TILES], F32, name="row_maxima")
+            live[("shift", u)] = small.tile([P, TILES], F32, name="shift")
+            live[("sum", u)] = small.tile([P, TILES], F32, name="row_sums")
+            live[("inv", u)] = small.tile([P, TILES], F32, name="inv_sums")
+
+        def is_unit(u):
+            return 0 <= u < UNITS
+
+        bias_f32 = const.tile([P, CIN], F32, name="bias_f32")
+        nc.vector.tensor_copy(out=bias_f32[:], in_=bias_bf[:])
+        w_grouped = const.tile([P, CIN * PACK], BF16, name="w_grouped", align_bytes=64)
+        for a in range(PACK):
+            wT_ps = psum.tile([P, PACK, P], BF16, name="wT_ps", tag="eT", bufs=2)
+            for j in range(PACK):
+                nc.tensor.transpose(wT_ps[:, j, :], wv_sb[:, a, j * P : (j + 1) * P], ident_bf[:])
+            nc.vector.tensor_copy(
+                out=w_grouped[:, a * P * PACK : (a + 1) * P * PACK].rearrange("p (o j) -> p o j", j=PACK),
+                in_=wT_ps[:].rearrange("p j o -> p o j"),
+            )
+        w_codes = const.tile([P, CIN], U32, name="w_codes", align_bytes=64)
+        w_scales = const.tile([P, CIN], U8, name="w_scales", align_bytes=64)
+        nc.vector.quantize_mx(out=w_codes[:].bitcast(FP8X4), scales=w_scales[:], in_=w_grouped[:])
+        quantise_group(0)
+
+        for s in range(-1, UNITS + 1):
+            if is_unit(s - 1):
+                attend(s - 1)
+            if is_unit(s + 1):
+                open_unit(s + 1)
+                project_v(s + 1)
+            if is_unit(s - 1):
+                normalise(s - 1)
+            if is_unit(s):
+                exp_tile(s, 0)
+                exp_tile(s, 1)
+                transpose_e(s, 0)
+            if is_unit(s + 1):
+                live[("s1", s + 1)] = psum.tile([P, 2 * P], F32, name="s1_ps", tag="s1")
+                scores(s + 1, 1)
+                row_max(s + 1, 1)
+            if is_unit(s - 1):
+                transpose_out(s - 1)
+            if is_unit(s):
+                exp_tile(s, 2)
+            if is_unit(s + 1):
+                live[("s20", s + 1)] = psum.tile([P, T], F32, name="s20_ps", tag="s20")
+                scores(s + 1, 0)
+                scores(s + 1, 2)
+                row_max(s + 1, 0)
+                row_max(s + 1, 2)
+            if is_unit(s):
+                exp_tile(s, 3)
+                transpose_e(s, 1)
+                nc.vector.reciprocal(live[("inv", s)][:], live[("sum", s)][:])
+            if is_unit(s + 1):
+                live[("s3", s + 1)] = psum.tile([P, T], F32, name="s3_ps", tag="s3")
+                scores(s + 1, 3)
+                row_max(s + 1, 3)
+                nc.vector.tensor_scalar_mul(
+                    out=live[("shift", s + 1)][:], in0=live[("max", s + 1)][:], scalar1=-SCALE
+                )
+            if is_unit(s):
+                regroup_e(s, 0)
+                regroup_e(s, 1)
+            if is_unit(s - 1):
+                store(s - 1)
+            if is_unit(s):
+                quantise_e(s)
+            if is_unit(s + 2) and (s + 2) % HEADS == 0:
+                quantise_group((s + 2) // HEADS)

@@ -19,9 +19,12 @@ BATCH, NODES, HEADS, T, DH = 2, 4, 4, 512, 128
 CIN = 512
 TILES = T // P
 HALF = T // 2
-UNITS = BATCH * NODES * HEADS
+GROUPS = BATCH * NODES
+UNITS = GROUPS * HEADS
+LOADS_AHEAD = 3
 SCALE = 1.0 / math.sqrt(DH)
 MASKED = -(2.0**30)
+BANKS = ((1,), (0, 2), (3,))
 
 FLOPS = 3 * 2 * BATCH * NODES * T * CIN * CIN
 
@@ -30,23 +33,29 @@ def tile_tatt_pa_t_kernel(tc, x, tem_embedding, Wv, bv, q, k, out):
     nc = tc.nc
     with ExitStack() as ctx:
         const = ctx.enter_context(tc.tile_pool(name="const", bufs=1))
-        loads = ctx.enter_context(tc.tile_pool(name="loads", bufs=BATCH * NODES))
+        loads = ctx.enter_context(tc.tile_pool(name="loads", bufs=GROUPS))
         work = ctx.enter_context(tc.tile_pool(name="work", bufs=2))
         small = ctx.enter_context(tc.tile_pool(name="small", bufs=4))
         psum = ctx.enter_context(tc.psum_pool(name="psum", bufs=1))
+        ctx.enter_context(tc.manual_schedule())
 
-        q_sb, k_sb, x_sb = [], [], []
-        wv_sb = const.tile([P, PACK, CIN], BF16, name="wv_sb")
-        bias_bf = const.tile([P, CIN], BF16, name="bias_bf")
-        for group in range(BATCH * NODES):
+        live = {}
+
+        def unit_of(u):
+            group, h = divmod(u, HEADS)
+            b, n = divmod(group, NODES)
+            return group, b, n, h
+
+        def is_unit(u):
+            return 0 <= u < UNITS
+
+        def load_group(group):
             b, n = divmod(group, NODES)
             q_g = loads.tile([P, HEADS, T], BF16, name="q_g")
             k_g = loads.tile([P, HEADS, T], BF16, name="k_g")
             x_g = loads.tile([P, PACK, T], BF16, name="x_g")
             nc.sync.dma_start(out=q_g[:], in_=q[b, :, n, :].rearrange("(h c) t -> c h t", c=P))
             nc.sync.dma_start(out=k_g[:], in_=k[b, :, n, :].rearrange("(h c) t -> c h t", c=P))
-            if group == 0:
-                nc.sync.dma_start(out=wv_sb[:], in_=Wv.rearrange("(a o) c -> o a c", o=P))
             nc.sync.dma_start(
                 out=x_g[:, 0:2, :], in_=x[b, :, n, :].rearrange("(j p) t -> p j t", p=P)
             )
@@ -54,16 +63,23 @@ def tile_tatt_pa_t_kernel(tc, x, tem_embedding, Wv, bv, q, k, out):
                 out=x_g[:, 2:4, :],
                 in_=tem_embedding[b, :, n, :].rearrange("(j p) t -> p j t", p=P),
             )
-            if group == 0:
-                nc.sync.dma_start(out=bias_bf[:], in_=bv.partition_broadcast(P))
-            q_sb.append(q_g)
-            k_sb.append(k_g)
-            x_sb.append(x_g)
+            live[("q", group)] = q_g
+            live[("k", group)] = k_g
+            live[("x", group)] = x_g
 
+        wv_sb = const.tile([P, PACK, CIN], BF16, name="wv_sb")
+        nc.sync.dma_start(out=wv_sb[:], in_=Wv.rearrange("(a o) c -> o a c", o=P))
+        load_group(0)
+        bias_bf = const.tile([P, CIN], BF16, name="bias_bf")
+        nc.sync.dma_start(out=bias_bf[:], in_=bv.partition_broadcast(P))
+        for group in range(1, LOADS_AHEAD):
+            load_group(group)
+
+        warm = const.tile([P, 2], F32, name="warm")
+        nc.vector.memset(warm[:], 0.0)
+        nc.scalar.activation(out=warm[:, 1:2], in_=warm[:, 0:1], func=ACT.Exp)
         ident_bf = const.tile([P, P], BF16, name="ident_bf")
         make_identity(nc, ident_bf[:])
-        ident_f32 = const.tile([P, P], F32, name="ident_f32")
-        make_identity(nc, ident_f32[:])
         mask_f32 = const.tile([P, P], F32, name="mask_f32")
         nc.gpsimd.memset(mask_f32[:], 0.0)
         nc.gpsimd.affine_select(
@@ -77,51 +93,76 @@ def tile_tatt_pa_t_kernel(tc, x, tem_embedding, Wv, bv, q, k, out):
         )
         mask_bf = const.tile([P, P], BF16, name="mask_bf")
         nc.vector.tensor_copy(out=mask_bf[:], in_=mask_f32[:])
+        ident_f32 = const.tile([P, P], F32, name="ident_f32")
+        make_identity(nc, ident_f32[:])
         e_ring = []
         for r in range(2):
             e_r = const.tile([P, TILES * T], BF16, name="e_ring%d" % r)
-            nc.gpsimd.memset(e_r[:], 0.0)
+            nc.vector.memset(e_r[:], 0.0)
             e_ring.append(e_r)
 
-        live = {}
-
-        def unit_of(u):
-            group, h = divmod(u, HEADS)
-            b, n = divmod(group, NODES)
-            return group, b, n, h
-
-        def score_region(u, i):
-            if i == 3:
-                return live[("s3", u)][:, :]
-            if i == 2:
-                return live[("s20", u)][:, 0 : 3 * P]
-            if i == 0:
-                return live[("s20", u)][:, 3 * P : 4 * P]
-            return live[("s1", u)][:, :]
-
-        def scores(u, i):
-            group, b, n, h = unit_of(u)
-            region = score_region(u, i)
-            q_i = q_sb[group][:, h, i * P : (i + 1) * P]
-            diagonal = region[:, i * P : (i + 1) * P]
-            nc.tensor.matmul(diagonal, lhsT=ident_bf[:], rhs=mask_bf[:], start=True, stop=False)
-            nc.tensor.matmul(
-                diagonal, lhsT=q_i, rhs=k_sb[group][:, h, i * P : (i + 1) * P], start=False, stop=True
+        w_grouped = const.tile([P, CIN * PACK], BF16, name="w_grouped", align_bytes=64)
+        for pair in range(2):
+            wT_ps = psum.tile([P, 2, PACK, P], BF16, name="wT_ps", tag="oT" if pair == 0 else "o")
+            for a in range(2):
+                for j in range(PACK):
+                    nc.tensor.transpose(
+                        wT_ps[:, a, j, :], wv_sb[:, 2 * pair + a, j * P : (j + 1) * P], ident_bf[:]
+                    )
+            nc.scalar.copy(
+                out=w_grouped[:, pair * 2 * P * PACK : (pair + 1) * 2 * P * PACK].rearrange(
+                    "p (a o j) -> p a o j", a=2, j=PACK
+                ),
+                in_=wT_ps[:].rearrange("p a j o -> p a o j"),
             )
-            if i > 0:
-                nc.tensor.matmul(
-                    region[:, 0 : i * P], lhsT=q_i, rhs=k_sb[group][:, h, 0 : i * P], start=True, stop=True
-                )
+        w_codes = const.tile([P, CIN], U32, name="w_codes", align_bytes=64)
+        w_scales = const.tile([P, CIN], U8, name="w_scales", align_bytes=64)
 
-        def row_max(u, i):
-            nc.vector.tensor_reduce(
-                out=live[("max", u)][:, i : i + 1], in_=score_region(u, i), axis=AXIS.X, op=ALU.max
+        eT_low = psum.tile([P, 2, HALF], F32, name="eT_low", tag="eT_low")
+        for ii in range(2):
+            nc.tensor.transpose(
+                eT_low[:, 1, ii * P : (ii + 1) * P], e_ring[0][:].bitcast(F32)[:, 0:P], ident_f32[:]
+            )
+
+        def open_unit(u):
+            live[("max", u)] = small.tile([P, TILES], F32, name="row_maxima")
+            live[("shift", u)] = small.tile([P, TILES], F32, name="shift")
+            live[("sum", u)] = small.tile([P, TILES], F32, name="row_sums")
+            live[("inv", u)] = small.tile([P, TILES], F32, name="inv_sums")
+
+        def scores(u, bank):
+            group, b, n, h = unit_of(u)
+            q_h = live[("q", group)][:, h, :]
+            k_h = live[("k", group)][:, h, :]
+            s_ps = psum.tile([P, T], F32, name="s_ps", tag="s%d" % bank)
+            first = 0
+            for i in BANKS[bank]:
+                region = s_ps[:, first : first + (i + 1) * P]
+                first += (i + 1) * P
+                live[("s", u, i)] = region
+                q_i = q_h[:, i * P : (i + 1) * P]
+                diagonal = region[:, i * P : (i + 1) * P]
+                nc.tensor.matmul(diagonal, lhsT=ident_bf[:], rhs=mask_bf[:], start=True, stop=False)
+                nc.tensor.matmul(
+                    diagonal, lhsT=q_i, rhs=k_h[:, i * P : (i + 1) * P], start=False, stop=True
+                )
+                if i > 0:
+                    nc.tensor.matmul(
+                        region[:, 0 : i * P], lhsT=q_i, rhs=k_h[:, 0 : i * P], start=True, stop=True
+                    )
+            for i in BANKS[bank]:
+                nc.vector.tensor_reduce(
+                    out=live[("max", u)][:, i : i + 1], in_=live[("s", u, i)], axis=AXIS.X, op=ALU.max
+                )
+            columns = slice(BANKS[bank][0], BANKS[bank][-1] + 1, 2)
+            nc.vector.tensor_scalar_mul(
+                out=live[("shift", u)][:, columns], in0=live[("max", u)][:, columns], scalar1=-SCALE
             )
 
         def exp_tile(u, i):
             nc.scalar.activation(
                 out=e_ring[u % 2][:, i * T : i * T + (i + 1) * P],
-                in_=score_region(u, i),
+                in_=live[("s", u, i)],
                 func=ACT.Exp,
                 bias=live[("shift", u)][:, i : i + 1],
                 scale=SCALE,
@@ -130,8 +171,11 @@ def tile_tatt_pa_t_kernel(tc, x, tem_embedding, Wv, bv, q, k, out):
 
         def transpose_e(u, half):
             e_words = e_ring[u % 2][:].bitcast(F32)
-            eT_ps = psum.tile([P, 2, HALF], F32, name="eT_ps", tag="eT", bufs=2)
-            for g in range(2):
+            if half == 0:
+                eT_ps = eT_low
+            else:
+                eT_ps = psum.tile([P, 2, HALF], F32, name="eT_high", tag="eT_high")
+            for g in range(half + 1):
                 for ii in range(2):
                     i = 2 * half + ii
                     nc.tensor.transpose(
@@ -143,8 +187,7 @@ def tile_tatt_pa_t_kernel(tc, x, tem_embedding, Wv, bv, q, k, out):
 
         def regroup_e(u, half):
             if half == 0:
-                e_grouped = work.tile([P, T * PACK], BF16, name="e_grouped", align_bytes=64)
-                live[("eg", u)] = e_grouped
+                live[("eg", u)] = work.tile([P, T * PACK], BF16, name="e_grouped", align_bytes=64)
             words = live[("eg", u)][:].bitcast(F32)[:, half * T : (half + 1) * T]
             nc.scalar.copy(
                 out=words.rearrange("p (t g) -> p t g", g=2),
@@ -161,7 +204,7 @@ def tile_tatt_pa_t_kernel(tc, x, tem_embedding, Wv, bv, q, k, out):
 
         def quantise_group(group):
             x_grouped = work.tile([P, T * PACK], BF16, name="x_grouped", align_bytes=64)
-            src = x_sb[group][:].rearrange("p j (g w r) -> p g r w j", g=2, w=P, r=2)
+            src = live[("x", group)][:].rearrange("p j (g w r) -> p g r w j", g=2, w=P, r=2)
             dst = x_grouped[:].rearrange("p (g r w j) -> p g r w j", g=2, r=2, w=P, j=PACK)
             for g in range(2):
                 nc.vector.tensor_copy(out=dst[:, g], in_=src[:, g])
@@ -223,10 +266,9 @@ def tile_tatt_pa_t_kernel(tc, x, tem_embedding, Wv, bv, q, k, out):
             live[("or", u)] = o_rows
 
         def transpose_out(u):
-            o_rows = live[("or", u)]
             o_ps = psum.tile([P, T], F32, name="o_ps", tag="o")
             for i in range(TILES):
-                nc.tensor.transpose(o_ps[:, i * P : (i + 1) * P], o_rows[:, i, :], ident_f32[:])
+                nc.tensor.transpose(o_ps[:, i * P : (i + 1) * P], live[("or", u)][:, i, :], ident_f32[:])
             live[("o", u)] = o_ps
 
         def store(u):
@@ -235,74 +277,51 @@ def tile_tatt_pa_t_kernel(tc, x, tem_embedding, Wv, bv, q, k, out):
             nc.scalar.copy(out=o_sb[:], in_=live[("o", u)][:])
             nc.sync.dma_start(out=out[b, h * DH : (h + 1) * DH, n, :], in_=o_sb[:])
 
-        def open_unit(u):
-            live[("max", u)] = small.tile([P, TILES], F32, name="row_maxima")
-            live[("shift", u)] = small.tile([P, TILES], F32, name="shift")
-            live[("sum", u)] = small.tile([P, TILES], F32, name="row_sums")
-            live[("inv", u)] = small.tile([P, TILES], F32, name="inv_sums")
-
-        def is_unit(u):
-            return 0 <= u < UNITS
-
+        open_unit(0)
+        for bank in range(len(BANKS)):
+            scores(0, bank)
         bias_f32 = const.tile([P, CIN], F32, name="bias_f32")
         nc.vector.tensor_copy(out=bias_f32[:], in_=bias_bf[:])
-        w_grouped = const.tile([P, CIN * PACK], BF16, name="w_grouped", align_bytes=64)
-        for a in range(PACK):
-            wT_ps = psum.tile([P, PACK, P], BF16, name="wT_ps", tag="eT", bufs=2)
-            for j in range(PACK):
-                nc.tensor.transpose(wT_ps[:, j, :], wv_sb[:, a, j * P : (j + 1) * P], ident_bf[:])
-            nc.vector.tensor_copy(
-                out=w_grouped[:, a * P * PACK : (a + 1) * P * PACK].rearrange("p (o j) -> p o j", j=PACK),
-                in_=wT_ps[:].rearrange("p j o -> p o j"),
-            )
-        w_codes = const.tile([P, CIN], U32, name="w_codes", align_bytes=64)
-        w_scales = const.tile([P, CIN], U8, name="w_scales", align_bytes=64)
         nc.vector.quantize_mx(out=w_codes[:].bitcast(FP8X4), scales=w_scales[:], in_=w_grouped[:])
         quantise_group(0)
 
-        for s in range(-1, UNITS + 1):
-            if is_unit(s - 1):
-                attend(s - 1)
+        for s in range(UNITS + 1):
+            if s % HEADS == 0 and s // HEADS + LOADS_AHEAD < GROUPS:
+                load_group(s // HEADS + LOADS_AHEAD)
             if is_unit(s + 1):
                 open_unit(s + 1)
-                project_v(s + 1)
             if is_unit(s - 1):
+                attend(s - 1)
                 normalise(s - 1)
             if is_unit(s):
-                exp_tile(s, 0)
                 exp_tile(s, 1)
-                transpose_e(s, 0)
             if is_unit(s + 1):
-                live[("s1", s + 1)] = psum.tile([P, 2 * P], F32, name="s1_ps", tag="s1")
-                scores(s + 1, 1)
-                row_max(s + 1, 1)
+                scores(s + 1, 0)
+            if is_unit(s):
+                exp_tile(s, 0)
+                transpose_e(s, 0)
             if is_unit(s - 1):
                 transpose_out(s - 1)
             if is_unit(s):
                 exp_tile(s, 2)
             if is_unit(s + 1):
-                live[("s20", s + 1)] = psum.tile([P, T], F32, name="s20_ps", tag="s20")
-                scores(s + 1, 0)
-                scores(s + 1, 2)
-                row_max(s + 1, 0)
-                row_max(s + 1, 2)
+                scores(s + 1, 1)
             if is_unit(s):
                 exp_tile(s, 3)
                 transpose_e(s, 1)
-                nc.vector.reciprocal(live[("inv", s)][:], live[("sum", s)][:])
             if is_unit(s + 1):
-                live[("s3", s + 1)] = psum.tile([P, T], F32, name="s3_ps", tag="s3")
-                scores(s + 1, 3)
-                row_max(s + 1, 3)
-                nc.vector.tensor_scalar_mul(
-                    out=live[("shift", s + 1)][:], in0=live[("max", s + 1)][:], scalar1=-SCALE
-                )
+                scores(s + 1, 2)
             if is_unit(s):
                 regroup_e(s, 0)
                 regroup_e(s, 1)
             if is_unit(s - 1):
                 store(s - 1)
             if is_unit(s):
+                nc.vector.reciprocal(live[("inv", s)][:], live[("sum", s)][:])
                 quantise_e(s)
+            if s == 0:
+                project_v(0)
+            if is_unit(s + 1):
+                project_v(s + 1)
             if is_unit(s + 2) and (s + 2) % HEADS == 0:
                 quantise_group((s + 2) // HEADS)

@@ -54,8 +54,6 @@ def tile_tatt_pa_t_kernel(tc, x, tem_embedding, Wv, bv, q, k, out):
             q_g = loads.tile([P, HEADS, T], BF16, name="q_g")
             k_g = loads.tile([P, HEADS, T], BF16, name="k_g")
             x_g = loads.tile([P, PACK, T], BF16, name="x_g")
-            nc.sync.dma_start(out=q_g[:], in_=q[b, :, n, :].rearrange("(h c) t -> c h t", c=P))
-            nc.sync.dma_start(out=k_g[:], in_=k[b, :, n, :].rearrange("(h c) t -> c h t", c=P))
             nc.sync.dma_start(
                 out=x_g[:, 0:2, :], in_=x[b, :, n, :].rearrange("(j p) t -> p j t", p=P)
             )
@@ -63,16 +61,17 @@ def tile_tatt_pa_t_kernel(tc, x, tem_embedding, Wv, bv, q, k, out):
                 out=x_g[:, 2:4, :],
                 in_=tem_embedding[b, :, n, :].rearrange("(j p) t -> p j t", p=P),
             )
+            nc.sync.dma_start(out=q_g[:], in_=q[b, :, n, :].rearrange("(h c) t -> c h t", c=P))
+            nc.sync.dma_start(out=k_g[:], in_=k[b, :, n, :].rearrange("(h c) t -> c h t", c=P))
             live[("q", group)] = q_g
             live[("k", group)] = k_g
             live[("x", group)] = x_g
 
         wv_sb = const.tile([P, PACK, CIN], BF16, name="wv_sb")
         nc.sync.dma_start(out=wv_sb[:], in_=Wv.rearrange("(a o) c -> o a c", o=P))
-        load_group(0)
         bias_bf = const.tile([P, CIN], BF16, name="bias_bf")
         nc.sync.dma_start(out=bias_bf[:], in_=bv.partition_broadcast(P))
-        for group in range(1, LOADS_AHEAD):
+        for group in range(LOADS_AHEAD):
             load_group(group)
 
         warm = const.tile([P, 2], F32, name="warm")
@@ -234,9 +233,12 @@ def tile_tatt_pa_t_kernel(tc, x, tem_embedding, Wv, bv, q, k, out):
                 in1=bias_f32[:, h * DH : (h + 1) * DH].unsqueeze(2).to_broadcast([P, DH, PACK]),
                 op=ALU.add,
             )
+            live[("vg", u)] = v_grouped
+
+        def quantise_v(u):
             v_codes = work.tile([P, DH], U32, name="v_codes", align_bytes=64, bufs=3)
             v_scales = work.tile([P, DH], U8, name="v_scales", align_bytes=64, bufs=3)
-            nc.vector.quantize_mx(out=v_codes[:].bitcast(FP8X4), scales=v_scales[:], in_=v_grouped[:])
+            nc.vector.quantize_mx(out=v_codes[:].bitcast(FP8X4), scales=v_scales[:], in_=live[("vg", u)][:])
             live[("vc", u)] = (v_codes, v_scales)
 
         def attend(u):
@@ -277,31 +279,30 @@ def tile_tatt_pa_t_kernel(tc, x, tem_embedding, Wv, bv, q, k, out):
             nc.scalar.copy(out=o_sb[:], in_=live[("o", u)][:])
             nc.sync.dma_start(out=out[b, h * DH : (h + 1) * DH, n, :], in_=o_sb[:])
 
-        open_unit(0)
-        for bank in range(len(BANKS)):
-            scores(0, bank)
         bias_f32 = const.tile([P, CIN], F32, name="bias_f32")
         nc.vector.tensor_copy(out=bias_f32[:], in_=bias_bf[:])
-        nc.vector.quantize_mx(out=w_codes[:].bitcast(FP8X4), scales=w_scales[:], in_=w_grouped[:])
         quantise_group(0)
+        nc.vector.quantize_mx(out=w_codes[:].bitcast(FP8X4), scales=w_scales[:], in_=w_grouped[:])
 
-        for s in range(UNITS + 1):
+        for s in range(-1, UNITS + 2):
             if s % HEADS == 0 and s // HEADS + LOADS_AHEAD < GROUPS:
                 load_group(s // HEADS + LOADS_AHEAD)
+            if is_unit(s - 1):
+                quantise_e(s - 1)
             if is_unit(s + 1):
                 open_unit(s + 1)
-            if is_unit(s - 1):
-                attend(s - 1)
-                normalise(s - 1)
+                project_v(s + 1)
             if is_unit(s):
                 exp_tile(s, 1)
             if is_unit(s + 1):
                 scores(s + 1, 0)
+                quantise_v(s + 1)
             if is_unit(s):
                 exp_tile(s, 0)
                 transpose_e(s, 0)
             if is_unit(s - 1):
-                transpose_out(s - 1)
+                attend(s - 1)
+                normalise(s - 1)
             if is_unit(s):
                 exp_tile(s, 2)
             if is_unit(s + 1):
@@ -309,19 +310,15 @@ def tile_tatt_pa_t_kernel(tc, x, tem_embedding, Wv, bv, q, k, out):
             if is_unit(s):
                 exp_tile(s, 3)
                 transpose_e(s, 1)
+                nc.vector.reciprocal(live[("inv", s)][:], live[("sum", s)][:])
+            if is_unit(s - 2):
+                store(s - 2)
             if is_unit(s + 1):
                 scores(s + 1, 2)
+            if is_unit(s - 1):
+                transpose_out(s - 1)
             if is_unit(s):
                 regroup_e(s, 0)
                 regroup_e(s, 1)
-            if is_unit(s - 1):
-                store(s - 1)
-            if is_unit(s):
-                nc.vector.reciprocal(live[("inv", s)][:], live[("sum", s)][:])
-                quantise_e(s)
-            if s == 0:
-                project_v(0)
-            if is_unit(s + 1):
-                project_v(s + 1)
-            if is_unit(s + 2) and (s + 2) % HEADS == 0:
-                quantise_group((s + 2) // HEADS)
+            if is_unit(s + 3) and (s + 3) % HEADS == 0:
+                quantise_group((s + 3) // HEADS)

@@ -21,6 +21,7 @@ TILES = T // P
 HALF = T // 2
 GROUPS = BATCH * NODES
 UNITS = GROUPS * HEADS
+E_RING = 3
 LOADS_AHEAD = 3
 SCALE = 1.0 / math.sqrt(DH)
 MASKED = -(2.0**30)
@@ -35,7 +36,7 @@ def tile_tatt_pa_t_kernel(tc, x, tem_embedding, Wv, bv, q, k, out):
         const = ctx.enter_context(tc.tile_pool(name="const", bufs=1))
         loads = ctx.enter_context(tc.tile_pool(name="loads", bufs=GROUPS))
         work = ctx.enter_context(tc.tile_pool(name="work", bufs=2))
-        small = ctx.enter_context(tc.tile_pool(name="small", bufs=4))
+        small = ctx.enter_context(tc.tile_pool(name="small", bufs=6))
         psum = ctx.enter_context(tc.psum_pool(name="psum", bufs=1))
         ctx.enter_context(tc.manual_schedule())
 
@@ -95,7 +96,7 @@ def tile_tatt_pa_t_kernel(tc, x, tem_embedding, Wv, bv, q, k, out):
         ident_f32 = const.tile([P, P], F32, name="ident_f32")
         make_identity(nc, ident_f32[:])
         e_ring = []
-        for r in range(2):
+        for r in range(E_RING):
             e_r = const.tile([P, TILES * T], BF16, name="e_ring%d" % r)
             nc.vector.memset(e_r[:], 0.0)
             e_ring.append(e_r)
@@ -124,12 +125,11 @@ def tile_tatt_pa_t_kernel(tc, x, tem_embedding, Wv, bv, q, k, out):
             )
 
         def open_unit(u):
-            live[("max", u)] = small.tile([P, TILES], F32, name="row_maxima")
             live[("shift", u)] = small.tile([P, TILES], F32, name="shift")
             live[("sum", u)] = small.tile([P, TILES], F32, name="row_sums")
             live[("inv", u)] = small.tile([P, TILES], F32, name="inv_sums")
 
-        def scores(u, bank):
+        def fill_scores(u, bank):
             group, b, n, h = unit_of(u)
             q_h = live[("q", group)][:, h, :]
             k_h = live[("k", group)][:, h, :]
@@ -138,7 +138,6 @@ def tile_tatt_pa_t_kernel(tc, x, tem_embedding, Wv, bv, q, k, out):
             for i in BANKS[bank]:
                 region = s_ps[:, first : first + (i + 1) * P]
                 first += (i + 1) * P
-                live[("s", u, i)] = region
                 q_i = q_h[:, i * P : (i + 1) * P]
                 diagonal = region[:, i * P : (i + 1) * P]
                 nc.tensor.matmul(diagonal, lhsT=ident_bf[:], rhs=mask_bf[:], start=True, stop=False)
@@ -149,27 +148,37 @@ def tile_tatt_pa_t_kernel(tc, x, tem_embedding, Wv, bv, q, k, out):
                     nc.tensor.matmul(
                         region[:, 0 : i * P], lhsT=q_i, rhs=k_h[:, 0 : i * P], start=True, stop=True
                     )
+            live[("s_ps", u, bank)] = s_ps
+
+        def scale_scores(u, bank):
+            s_sb = work.tile([P, T], F32, name="s_sb%d" % bank, bufs=3)
+            first = 0
             for i in BANKS[bank]:
-                nc.vector.tensor_reduce(
-                    out=live[("max", u)][:, i : i + 1], in_=live[("s", u, i)], axis=AXIS.X, op=ALU.max
+                columns = slice(first, first + (i + 1) * P)
+                first += (i + 1) * P
+                nc.vector.tensor_scalar(
+                    out=s_sb[:, columns],
+                    in0=live[("s_ps", u, bank)][:, columns],
+                    scalar1=-SCALE,
+                    scalar2=None,
+                    op0=ALU.mult,
+                    op1=ALU.min,
+                    accum_out=live[("shift", u)][:, i : i + 1],
                 )
-            columns = slice(BANKS[bank][0], BANKS[bank][-1] + 1, 2)
-            nc.vector.tensor_scalar_mul(
-                out=live[("shift", u)][:, columns], in0=live[("max", u)][:, columns], scalar1=-SCALE
-            )
+                live[("s", u, i)] = s_sb[:, columns]
 
         def exp_tile(u, i):
             nc.scalar.activation(
-                out=e_ring[u % 2][:, i * T : i * T + (i + 1) * P],
+                out=e_ring[u % E_RING][:, i * T : i * T + (i + 1) * P],
                 in_=live[("s", u, i)],
                 func=ACT.Exp,
                 bias=live[("shift", u)][:, i : i + 1],
-                scale=SCALE,
+                scale=-1.0,
                 accum_out=live[("sum", u)][:, i : i + 1],
             )
 
         def transpose_e(u, half):
-            e_words = e_ring[u % 2][:].bitcast(F32)
+            e_words = e_ring[u % E_RING][:].bitcast(F32)
             if half == 0:
                 eT_ps = eT_low
             else:
@@ -186,7 +195,9 @@ def tile_tatt_pa_t_kernel(tc, x, tem_embedding, Wv, bv, q, k, out):
 
         def regroup_e(u, half):
             if half == 0:
-                live[("eg", u)] = work.tile([P, T * PACK], BF16, name="e_grouped", align_bytes=64)
+                live[("eg", u)] = work.tile(
+                    [P, T * PACK], BF16, name="e_grouped", align_bytes=64, bufs=3
+                )
             words = live[("eg", u)][:].bitcast(F32)[:, half * T : (half + 1) * T]
             nc.scalar.copy(
                 out=words.rearrange("p (t g) -> p t g", g=2),
@@ -226,18 +237,22 @@ def tile_tatt_pa_t_kernel(tc, x, tem_embedding, Wv, bv, q, k, out):
                     start=True,
                     stop=True,
                 )
+            live[("v_ps", u)] = v_ps
+
+        def add_bias(u):
+            group, b, n, h = unit_of(u)
             v_grouped = work.tile([P, DH * PACK], BF16, name="v_grouped", align_bytes=64)
             nc.vector.tensor_tensor(
                 out=v_grouped[:].rearrange("p (c s) -> p c s", s=PACK),
-                in0=v_ps[:].rearrange("p s c -> p c s"),
+                in0=live[("v_ps", u)][:].rearrange("p s c -> p c s"),
                 in1=bias_f32[:, h * DH : (h + 1) * DH].unsqueeze(2).to_broadcast([P, DH, PACK]),
                 op=ALU.add,
             )
             live[("vg", u)] = v_grouped
 
         def quantise_v(u):
-            v_codes = work.tile([P, DH], U32, name="v_codes", align_bytes=64, bufs=3)
-            v_scales = work.tile([P, DH], U8, name="v_scales", align_bytes=64, bufs=3)
+            v_codes = work.tile([P, DH], U32, name="v_codes", align_bytes=64, bufs=4)
+            v_scales = work.tile([P, DH], U8, name="v_scales", align_bytes=64, bufs=4)
             nc.vector.quantize_mx(out=v_codes[:].bitcast(FP8X4), scales=v_scales[:], in_=live[("vg", u)][:])
             live[("vc", u)] = (v_codes, v_scales)
 
@@ -284,41 +299,47 @@ def tile_tatt_pa_t_kernel(tc, x, tem_embedding, Wv, bv, q, k, out):
         quantise_group(0)
         nc.vector.quantize_mx(out=w_codes[:].bitcast(FP8X4), scales=w_scales[:], in_=w_grouped[:])
 
-        for s in range(-1, UNITS + 2):
-            if s % HEADS == 0 and s // HEADS + LOADS_AHEAD < GROUPS:
+        for s in range(-3, UNITS + 3):
+            if s >= 0 and s % HEADS == 0 and s // HEADS + LOADS_AHEAD < GROUPS:
                 load_group(s // HEADS + LOADS_AHEAD)
+            if is_unit(s):
+                transpose_e(s, 0)
+                transpose_e(s, 1)
+            if is_unit(s + 1):
+                for tiles in BANKS:
+                    for i in tiles:
+                        exp_tile(s + 1, i)
+            if is_unit(s + 2):
+                open_unit(s + 2)
+                scale_scores(s + 2, 0)
+            if is_unit(s + 3):
+                fill_scores(s + 3, 0)
+            if is_unit(s - 2):
+                normalise(s - 2)
             if is_unit(s - 1):
                 quantise_e(s - 1)
-            if is_unit(s + 1):
-                open_unit(s + 1)
-                project_v(s + 1)
-            if is_unit(s):
-                exp_tile(s, 1)
-            if is_unit(s + 1):
-                scores(s + 1, 0)
-                quantise_v(s + 1)
-            if is_unit(s):
-                exp_tile(s, 0)
-                transpose_e(s, 0)
-            if is_unit(s - 1):
                 attend(s - 1)
-                normalise(s - 1)
-            if is_unit(s):
-                exp_tile(s, 2)
-            if is_unit(s + 1):
-                scores(s + 1, 1)
-            if is_unit(s):
-                exp_tile(s, 3)
-                transpose_e(s, 1)
-                nc.vector.reciprocal(live[("inv", s)][:], live[("sum", s)][:])
+            if is_unit(s - 3):
+                store(s - 3)
             if is_unit(s - 2):
-                store(s - 2)
+                transpose_out(s - 2)
+            if is_unit(s + 2):
+                scale_scores(s + 2, 1)
+            if is_unit(s + 3):
+                fill_scores(s + 3, 1)
             if is_unit(s + 1):
-                scores(s + 1, 2)
-            if is_unit(s - 1):
-                transpose_out(s - 1)
+                add_bias(s + 1)
+            if is_unit(s + 2):
+                project_v(s + 2)
             if is_unit(s):
                 regroup_e(s, 0)
                 regroup_e(s, 1)
-            if is_unit(s + 3) and (s + 3) % HEADS == 0:
-                quantise_group((s + 3) // HEADS)
+            if is_unit(s + 2):
+                scale_scores(s + 2, 2)
+            if is_unit(s + 3):
+                fill_scores(s + 3, 2)
+            if is_unit(s + 1):
+                quantise_v(s + 1)
+                nc.vector.reciprocal(live[("inv", s + 1)][:], live[("sum", s + 1)][:])
+            if is_unit(s + 5) and (s + 5) % HEADS == 0:
+                quantise_group((s + 5) // HEADS)

@@ -212,15 +212,27 @@ def tile_tatt_pa_t_kernel(tc, x, tem_embedding, Wv, bv, q, k, out):
             )
             live[("ec", u)] = (e_codes, e_scales)
 
-        def quantise_group(group):
-            x_grouped = work.tile([P, T * PACK], BF16, name="x_grouped", align_bytes=64)
-            src = live[("x", group)][:].rearrange("p j (g w r) -> p g r w j", g=2, w=P, r=2)
-            dst = x_grouped[:].rearrange("p (g r w j) -> p g r w j", g=2, r=2, w=P, j=PACK)
-            for g in range(2):
-                nc.vector.tensor_copy(out=dst[:, g], in_=src[:, g])
+        def regroup_x(engine, group, piece):
+            if piece == 0:
+                live[("xg", group)] = work.tile([P, T * PACK], BF16, name="x_grouped", align_bytes=64)
+            g, r = divmod(piece, 2)
+            engine.tensor_scalar(
+                out=live[("xg", group)][:, piece * P * PACK : (piece + 1) * P * PACK].rearrange(
+                    "p (w j) -> p w j", j=PACK
+                ),
+                in0=live[("x", group)][:].rearrange("p j (g w r) -> p g r w j", g=2, w=P, r=2)[:, g, r],
+                scalar1=1.0,
+                scalar2=0.0,
+                op0=ALU.mult,
+                op1=ALU.add,
+            )
+
+        def quantise_x(group):
             x_codes = work.tile([P, T], U32, name="x_codes", align_bytes=64)
             x_scales = work.tile([P, T], U8, name="x_scales", align_bytes=64)
-            nc.vector.quantize_mx(out=x_codes[:].bitcast(FP8X4), scales=x_scales[:], in_=x_grouped[:])
+            nc.vector.quantize_mx(
+                out=x_codes[:].bitcast(FP8X4), scales=x_scales[:], in_=live[("xg", group)][:]
+            )
             live[("xc", group)] = (x_codes, x_scales)
 
         def project_v(u):
@@ -296,12 +308,16 @@ def tile_tatt_pa_t_kernel(tc, x, tem_embedding, Wv, bv, q, k, out):
 
         bias_f32 = const.tile([P, CIN], F32, name="bias_f32")
         nc.vector.tensor_copy(out=bias_f32[:], in_=bias_bf[:])
-        quantise_group(0)
+        for piece in range(PACK):
+            regroup_x(nc.vector, 0, piece)
         nc.vector.quantize_mx(out=w_codes[:].bitcast(FP8X4), scales=w_scales[:], in_=w_grouped[:])
+        quantise_x(0)
 
-        for s in range(-3, UNITS + 3):
+        for s in range(-5, UNITS + 3):
             if s >= 0 and s % HEADS == 0 and s // HEADS + LOADS_AHEAD < GROUPS:
                 load_group(s // HEADS + LOADS_AHEAD)
+            if is_unit(s + 9):
+                regroup_x(nc.gpsimd, (s + 9) // HEADS, (s + 9) % HEADS)
             if is_unit(s):
                 transpose_e(s, 0)
                 transpose_e(s, 1)
@@ -342,4 +358,4 @@ def tile_tatt_pa_t_kernel(tc, x, tem_embedding, Wv, bv, q, k, out):
                 quantise_v(s + 1)
                 nc.vector.reciprocal(live[("inv", s + 1)][:], live[("sum", s + 1)][:])
             if is_unit(s + 5) and (s + 5) % HEADS == 0:
-                quantise_group((s + 5) // HEADS)
+                quantise_x((s + 5) // HEADS)

@@ -22,6 +22,7 @@ HALF = T // 2
 GROUPS = BATCH * NODES
 UNITS = GROUPS * HEADS
 E_RING = 3
+SCALAR_TAKES_EVERY = 3
 LOADS_AHEAD = 3
 SCALE = 1.0 / math.sqrt(DH)
 MASKED = -(2.0**30)
@@ -286,12 +287,21 @@ def tile_tatt_pa_t_kernel(tc, x, tem_embedding, Wv, bv, q, k, out):
 
         def normalise(u):
             o_rows = work.tile([P, TILES, DH], F32, name="o_rows")
-            nc.vector.tensor_tensor(
-                out=o_rows[:],
-                in0=live[("oT", u)][:],
-                in1=live[("inv", u)][:].unsqueeze(2).to_broadcast([P, TILES, DH]),
-                op=ALU.mult,
-            )
+            if u % SCALAR_TAKES_EVERY == SCALAR_TAKES_EVERY - 1:
+                for i in range(TILES):
+                    nc.scalar.activation(
+                        out=o_rows[:, i, :],
+                        in_=live[("oT", u)][:, i, :],
+                        func=ACT.Copy,
+                        scale=live[("inv", u)][:, i : i + 1],
+                    )
+            else:
+                nc.vector.tensor_tensor(
+                    out=o_rows[:],
+                    in0=live[("oT", u)][:],
+                    in1=live[("inv", u)][:].unsqueeze(2).to_broadcast([P, TILES, DH]),
+                    op=ALU.mult,
+                )
             live[("or", u)] = o_rows
 
         def transpose_out(u):

@@ -8,6 +8,7 @@ F32 = mybir.dt.float32
 BF16 = mybir.dt.bfloat16
 U32 = mybir.dt.uint32
 U8 = mybir.dt.uint8
+I32 = mybir.dt.int32
 FP8X4 = mybir.dt.float8_e4m3fn_x4
 ALU = mybir.AluOpType
 ACT = mybir.ActivationFunctionType
@@ -18,11 +19,11 @@ PACK = 4
 BATCH, NODES, HEADS, T, DH = 2, 4, 4, 512, 128
 CIN = 512
 TILES = T // P
-HALF = T // 2
 GROUPS = BATCH * NODES
 UNITS = GROUPS * HEADS
-E_RING = 3
-SCALAR_TAKES_EVERY = 3
+V_WORDS = DH + DH // PACK
+V_RING = 3
+FOR_TILE_2, FOR_TILE_0, FOR_TILE_1 = range(3)
 LOADS_AHEAD = 3
 SCALE = 1.0 / math.sqrt(DH)
 MASKED = -(2.0**30)
@@ -70,10 +71,26 @@ def tile_tatt_pa_t_kernel(tc, x, tem_embedding, Wv, bv, q, k, out):
             live[("x", group)] = x_g
 
         wv_sb = const.tile([P, PACK, CIN], BF16, name="wv_sb")
-        nc.sync.dma_start(out=wv_sb[:], in_=Wv.rearrange("(a o) c -> o a c", o=P))
         bias_bf = const.tile([P, CIN], BF16, name="bias_bf")
+        q_g = loads.tile([P, HEADS, T], BF16, name="q_g")
+        k_g = loads.tile([P, HEADS, T], BF16, name="k_g")
+        x_g = loads.tile([P, PACK, T], BF16, name="x_g")
+        q_0 = q[0, :, 0, :].rearrange("(h c) t -> c h t", c=P)
+        k_0 = k[0, :, 0, :].rearrange("(h c) t -> c h t", c=P)
+        nc.sync.dma_start(out=q_g[:, 0:1, :], in_=q_0[:, 0:1, :])
+        nc.sync.dma_start(out=k_g[:, 0:1, :], in_=k_0[:, 0:1, :])
+        nc.sync.dma_start(out=wv_sb[:], in_=Wv.rearrange("(a o) c -> o a c", o=P))
+        nc.sync.dma_start(out=x_g[:, 0:2, :], in_=x[0, :, 0, :].rearrange("(j p) t -> p j t", p=P))
+        nc.sync.dma_start(
+            out=x_g[:, 2:4, :], in_=tem_embedding[0, :, 0, :].rearrange("(j p) t -> p j t", p=P)
+        )
+        nc.sync.dma_start(out=q_g[:, 1:HEADS, :], in_=q_0[:, 1:HEADS, :])
+        nc.sync.dma_start(out=k_g[:, 1:HEADS, :], in_=k_0[:, 1:HEADS, :])
         nc.sync.dma_start(out=bias_bf[:], in_=bv.partition_broadcast(P))
-        for group in range(LOADS_AHEAD):
+        live[("q", 0)] = q_g
+        live[("k", 0)] = k_g
+        live[("x", 0)] = x_g
+        for group in range(1, LOADS_AHEAD):
             load_group(group)
 
         warm = const.tile([P, 2], F32, name="warm")
@@ -81,49 +98,31 @@ def tile_tatt_pa_t_kernel(tc, x, tem_embedding, Wv, bv, q, k, out):
         nc.scalar.activation(out=warm[:, 1:2], in_=warm[:, 0:1], func=ACT.Exp)
         ident_bf = const.tile([P, P], BF16, name="ident_bf")
         make_identity(nc, ident_bf[:])
-        mask_f32 = const.tile([P, P], F32, name="mask_f32")
-        nc.gpsimd.memset(mask_f32[:], 0.0)
+        mask_bf = const.tile([P, P], BF16, name="mask_bf")
+        nc.gpsimd.memset(mask_bf[:], 0.0)
         nc.gpsimd.affine_select(
-            out=mask_f32[:],
-            in_=mask_f32[:],
+            out=mask_bf[:],
+            in_=mask_bf[:],
             compare_op=ALU.is_ge,
             fill=MASKED,
             base=0,
             pattern=[[-1, P]],
             channel_multiplier=1,
         )
-        mask_bf = const.tile([P, P], BF16, name="mask_bf")
-        nc.vector.tensor_copy(out=mask_bf[:], in_=mask_f32[:])
         ident_f32 = const.tile([P, P], F32, name="ident_f32")
         make_identity(nc, ident_f32[:])
-        e_ring = []
-        for r in range(E_RING):
-            e_r = const.tile([P, TILES * T], BF16, name="e_ring%d" % r)
-            nc.vector.memset(e_r[:], 0.0)
-            e_ring.append(e_r)
+        v_full, v_part = [], []
+        for r in range(V_RING):
+            v_f = const.tile([P, 2, V_WORDS], U32, name="v_full%d" % r, align_bytes=64)
+            nc.vector.memset(v_f[:, :, DH:V_WORDS].bitcast(I32), 0)
+            v_full.append(v_f)
+            v_p = const.tile([P, 2, 3, V_WORDS], U32, name="v_part%d" % r, align_bytes=64)
+            nc.gpsimd.memset(v_p[:].bitcast(I32), 0)
+            v_part.append(v_p)
 
         w_grouped = const.tile([P, CIN * PACK], BF16, name="w_grouped", align_bytes=64)
-        for pair in range(2):
-            wT_ps = psum.tile([P, 2, PACK, P], BF16, name="wT_ps", tag="oT" if pair == 0 else "o")
-            for a in range(2):
-                for j in range(PACK):
-                    nc.tensor.transpose(
-                        wT_ps[:, a, j, :], wv_sb[:, 2 * pair + a, j * P : (j + 1) * P], ident_bf[:]
-                    )
-            nc.scalar.copy(
-                out=w_grouped[:, pair * 2 * P * PACK : (pair + 1) * 2 * P * PACK].rearrange(
-                    "p (a o j) -> p a o j", a=2, j=PACK
-                ),
-                in_=wT_ps[:].rearrange("p a j o -> p a o j"),
-            )
         w_codes = const.tile([P, CIN], U32, name="w_codes", align_bytes=64)
         w_scales = const.tile([P, CIN], U8, name="w_scales", align_bytes=64)
-
-        eT_low = psum.tile([P, 2, HALF], F32, name="eT_low", tag="eT_low")
-        for ii in range(2):
-            nc.tensor.transpose(
-                eT_low[:, 1, ii * P : (ii + 1) * P], e_ring[0][:].bitcast(F32)[:, 0:P], ident_f32[:]
-            )
 
         def open_unit(u):
             live[("shift", u)] = small.tile([P, TILES], F32, name="shift")
@@ -158,8 +157,10 @@ def tile_tatt_pa_t_kernel(tc, x, tem_embedding, Wv, bv, q, k, out):
                 columns = slice(first, first + (i + 1) * P)
                 first += (i + 1) * P
                 nc.vector.tensor_scalar(
-                    out=s_sb[:, columns],
-                    in0=live[("s_ps", u, bank)][:, columns],
+                    out=s_sb[:, columns].rearrange("p (g w r) -> p g w r", g=2, r=2),
+                    in0=live[("s_ps", u, bank)][:, columns].rearrange(
+                        "p (w g r) -> p g w r", g=2, r=2
+                    ),
                     scalar1=-SCALE,
                     scalar2=None,
                     op0=ALU.mult,
@@ -168,60 +169,80 @@ def tile_tatt_pa_t_kernel(tc, x, tem_embedding, Wv, bv, q, k, out):
                 )
                 live[("s", u, i)] = s_sb[:, columns]
 
+        def open_e(u):
+            live[("e", u)] = work.tile([P, 2, 2, 2 * P], BF16, name="e_main", bufs=3)
+            if u % 2 == 0:
+                live[("e_pair", u // 2)] = work.tile([P, 2, 2 * P], BF16, name="e_pair")
+
         def exp_tile(u, i):
+            if i == 1:
+                e_tile, first = live[("e_pair", u // 2)][:], (u % 2) * P
+            elif i == 3:
+                e_tile, first = live[("e", u)][:, 0], 0
+            else:
+                e_tile, first = live[("e", u)][:, 1], 0 if i == 2 else 3 * P // 2
             nc.scalar.activation(
-                out=e_ring[u % E_RING][:, i * T : i * T + (i + 1) * P],
-                in_=live[("s", u, i)],
+                out=e_tile[:, :, first : first + (i + 1) * P // 2],
+                in_=live[("s", u, i)].rearrange("p (g x) -> p g x", g=2),
                 func=ACT.Exp,
                 bias=live[("shift", u)][:, i : i + 1],
                 scale=-1.0,
                 accum_out=live[("sum", u)][:, i : i + 1],
             )
 
-        def transpose_e(u, half):
-            e_words = e_ring[u % E_RING][:].bitcast(F32)
-            if half == 0:
-                eT_ps = eT_low
-            else:
-                eT_ps = psum.tile([P, 2, HALF], F32, name="eT_high", tag="eT_high")
-            for g in range(half + 1):
-                for ii in range(2):
-                    i = 2 * half + ii
-                    nc.tensor.transpose(
-                        eT_ps[:, g, ii * P : (ii + 1) * P],
-                        e_words[:, i * HALF + g * P : i * HALF + (g + 1) * P],
-                        ident_f32[:],
-                    )
-            live[("eT", u, half)] = eT_ps
+        def transpose_words(eT_ps, e_tile):
+            for g in range(2):
+                nc.tensor.transpose(eT_ps[:, g, :], e_tile[:, g, :].bitcast(F32), ident_f32[:])
 
-        def regroup_e(u, half):
-            if half == 0:
-                live[("eg", u)] = work.tile(
-                    [P, T * PACK], BF16, name="e_grouped", align_bytes=64, bufs=3
-                )
-            words = live[("eg", u)][:].bitcast(F32)[:, half * T : (half + 1) * T]
+        def transpose_e(u):
+            eT_ps = psum.tile([P, 2, 2, P], F32, name="eT_main", tag="eT_main")
+            for block in range(2):
+                transpose_words(eT_ps[:, block], live[("e", u)][:, block])
+            live[("eT", u)] = eT_ps
+
+        def transpose_pair(m):
+            eT_ps = psum.tile([P, 2, P], F32, name="eT_pair", tag="eT_pair")
+            transpose_words(eT_ps, live[("e_pair", m)])
+            live[("eT_pair", m)] = eT_ps
+
+        def regroup_e(u):
+            live[("eg", u)] = work.tile([P, 2 * P * PACK], BF16, name="e_grouped", align_bytes=64)
             nc.scalar.copy(
-                out=words.rearrange("p (t g) -> p t g", g=2),
-                in_=live[("eT", u, half)][:].rearrange("p g t -> p t g"),
+                out=live[("eg", u)][:].bitcast(F32).rearrange("p (k t g) -> p k t g", k=2, g=2),
+                in_=live[("eT", u)][:].rearrange("p k g t -> p k t g"),
+            )
+
+        def regroup_pair(m):
+            live[("eg_pair", m)] = work.tile([P, P * PACK], BF16, name="e_grouped_pair", align_bytes=64)
+            nc.scalar.copy(
+                out=live[("eg_pair", m)][:].bitcast(F32).rearrange("p (t g) -> p t g", g=2),
+                in_=live[("eT_pair", m)][:].rearrange("p g t -> p t g"),
             )
 
         def quantise_e(u):
-            e_codes = work.tile([P, T], U32, name="e_codes", align_bytes=64)
-            e_scales = work.tile([P, T], U8, name="e_scales", align_bytes=64)
+            e_codes = work.tile([P, 2 * P], U32, name="e_codes", align_bytes=64, bufs=3)
+            e_scales = work.tile([P, 2 * P], U8, name="e_scales", align_bytes=64, bufs=3)
             nc.vector.quantize_mx(
                 out=e_codes[:].bitcast(FP8X4), scales=e_scales[:], in_=live[("eg", u)][:]
             )
             live[("ec", u)] = (e_codes, e_scales)
 
+        def quantise_pair(m):
+            p_codes = work.tile([P, P], U32, name="p_codes", align_bytes=64)
+            p_scales = work.tile([P, P], U8, name="p_scales", align_bytes=64)
+            nc.vector.quantize_mx(
+                out=p_codes[:].bitcast(FP8X4), scales=p_scales[:], in_=live[("eg_pair", m)][:]
+            )
+            live[("pc", m)] = (p_codes, p_scales)
+
         def regroup_x(engine, group, piece):
             if piece == 0:
                 live[("xg", group)] = work.tile([P, T * PACK], BF16, name="x_grouped", align_bytes=64)
-            g, r = divmod(piece, 2)
             engine.tensor_scalar(
                 out=live[("xg", group)][:, piece * P * PACK : (piece + 1) * P * PACK].rearrange(
                     "p (w j) -> p w j", j=PACK
                 ),
-                in0=live[("x", group)][:].rearrange("p j (g w r) -> p g r w j", g=2, w=P, r=2)[:, g, r],
+                in0=live[("x", group)][:].rearrange("p j (w s) -> p s w j", s=PACK)[:, piece],
                 scalar1=1.0,
                 scalar2=0.0,
                 op0=ALU.mult,
@@ -258,28 +279,47 @@ def tile_tatt_pa_t_kernel(tc, x, tem_embedding, Wv, bv, q, k, out):
             nc.vector.tensor_tensor(
                 out=v_grouped[:].rearrange("p (c s) -> p c s", s=PACK),
                 in0=live[("v_ps", u)][:].rearrange("p s c -> p c s"),
-                in1=bias_f32[:, h * DH : (h + 1) * DH].unsqueeze(2).to_broadcast([P, DH, PACK]),
+                in1=bias_bf[:, h * DH : (h + 1) * DH].unsqueeze(2).to_broadcast([P, DH, PACK]),
                 op=ALU.add,
             )
             live[("vg", u)] = v_grouped
 
+        def mx_operand(words):
+            return words[:, 0:DH].bitcast(FP8X4), words[:, DH:V_WORDS].bitcast(U8)
+
         def quantise_v(u):
-            v_codes = work.tile([P, DH], U32, name="v_codes", align_bytes=64, bufs=4)
-            v_scales = work.tile([P, DH], U8, name="v_scales", align_bytes=64, bufs=4)
-            nc.vector.quantize_mx(out=v_codes[:].bitcast(FP8X4), scales=v_scales[:], in_=live[("vg", u)][:])
-            live[("vc", u)] = (v_codes, v_scales)
+            codes, scales = mx_operand(v_full[u // 2 % V_RING][:, u % 2, :])
+            nc.vector.quantize_mx(out=codes, scales=scales, in_=live[("vg", u)][:])
+
+        def spread_v(m):
+            v_f = v_full[m % V_RING][:].bitcast(I32)
+            v_p = v_part[m % V_RING][:].bitcast(I32)
+            nc.sync.dma_start(out=v_p[0:64, :, FOR_TILE_2, :], in_=v_f[0:64, :, :])
+            nc.sync.dma_start(out=v_p[64:96, :, FOR_TILE_2, :], in_=v_f[64:96, :, :])
+            nc.sync.dma_start(out=v_p[96:128, :, FOR_TILE_0, :], in_=v_f[0:32, :, :])
+            for odd in range(2):
+                rows = slice(64 * odd, 64 * odd + 64)
+                nc.sync.dma_start(out=v_p[rows, odd, FOR_TILE_1, :], in_=v_f[0:64, odd, :])
 
         def attend(u):
-            e_codes, e_scales = live[("ec", u)]
-            v_codes, v_scales = live[("vc", u)]
+            ring, odd = u // 2 % V_RING, u % 2
+            v_p = v_part[ring]
+            main = live[("ec", u)]
             oT_ps = psum.tile([P, TILES, DH], F32, name="oT_ps", tag="oT")
-            for i in range(TILES):
+            for i, e_tile, block, v_words in (
+                (3, main, 0, v_full[ring][:, odd, :]),
+                (2, main, 1, v_p[:, odd, FOR_TILE_2, :]),
+                (0, main, 1, v_p[:, odd, FOR_TILE_0, :]),
+                (1, live[("pc", u // 2)], 0, v_p[:, odd, FOR_TILE_1, :]),
+            ):
+                e_codes, e_scales = e_tile
+                v_codes, v_scales = mx_operand(v_words)
                 nc.tensor.matmul_mx(
                     out=oT_ps[:, i, :],
-                    lhsT=e_codes[:, i * P : (i + 1) * P].bitcast(FP8X4),
-                    lhsT_scale=e_scales[:, i * P : (i + 1) * P],
-                    rhs=v_codes[:].bitcast(FP8X4),
-                    rhs_scale=v_scales[:],
+                    lhsT=e_codes[:, block * P : (block + 1) * P].bitcast(FP8X4),
+                    lhsT_scale=e_scales[:, block * P : (block + 1) * P],
+                    rhs=v_codes,
+                    rhs_scale=v_scales,
                     start=True,
                     stop=True,
                 )
@@ -287,7 +327,7 @@ def tile_tatt_pa_t_kernel(tc, x, tem_embedding, Wv, bv, q, k, out):
 
         def normalise(u):
             o_rows = work.tile([P, TILES, DH], F32, name="o_rows")
-            if u % SCALAR_TAKES_EVERY == SCALAR_TAKES_EVERY - 1:
+            if u % 2 == 1:
                 for i in range(TILES):
                     nc.scalar.activation(
                         out=o_rows[:, i, :],
@@ -316,22 +356,41 @@ def tile_tatt_pa_t_kernel(tc, x, tem_embedding, Wv, bv, q, k, out):
             nc.scalar.copy(out=o_sb[:], in_=live[("o", u)][:])
             nc.sync.dma_start(out=out[b, h * DH : (h + 1) * DH, n, :], in_=o_sb[:])
 
-        bias_f32 = const.tile([P, CIN], F32, name="bias_f32")
-        nc.vector.tensor_copy(out=bias_f32[:], in_=bias_bf[:])
-        for piece in range(PACK):
-            regroup_x(nc.vector, 0, piece)
-        nc.vector.quantize_mx(out=w_codes[:].bitcast(FP8X4), scales=w_scales[:], in_=w_grouped[:])
-        quantise_x(0)
+        def regroup_w():
+            for pair in range(2):
+                wT_ps = psum.tile([P, 2, PACK, P], BF16, name="wT_ps", tag="oT" if pair == 0 else "o")
+                for a in range(2):
+                    for j in range(PACK):
+                        nc.tensor.transpose(
+                            wT_ps[:, a, j, :], wv_sb[:, 2 * pair + a, j * P : (j + 1) * P], ident_bf[:]
+                        )
+                copy = nc.scalar.copy if pair == 0 else nc.vector.tensor_copy
+                copy(
+                    out=w_grouped[:, pair * 2 * P * PACK : (pair + 1) * 2 * P * PACK].rearrange(
+                        "p (a o j) -> p a o j", a=2, j=PACK
+                    ),
+                    in_=wT_ps[:].rearrange("p a j o -> p a o j"),
+                )
 
-        for s in range(-5, UNITS + 3):
+        def prepare_projection():
+            for piece in range(PACK):
+                regroup_x(nc.vector if piece < 2 else nc.gpsimd, 0, piece)
+            for piece in range(2):
+                regroup_x(nc.gpsimd, 1, piece)
+            nc.vector.quantize_mx(out=w_codes[:].bitcast(FP8X4), scales=w_scales[:], in_=w_grouped[:])
+            quantise_x(0)
+
+        for s in range(-3, UNITS + 4):
             if s >= 0 and s % HEADS == 0 and s // HEADS + LOADS_AHEAD < GROUPS:
                 load_group(s // HEADS + LOADS_AHEAD)
-            if is_unit(s + 9):
-                regroup_x(nc.gpsimd, (s + 9) // HEADS, (s + 9) % HEADS)
+            if s >= -1 and is_unit(s + 7):
+                regroup_x(nc.gpsimd, (s + 7) // HEADS, (s + 7) % HEADS)
             if is_unit(s):
-                transpose_e(s, 0)
-                transpose_e(s, 1)
+                transpose_e(s)
+                if s % 2 == 1:
+                    transpose_pair(s // 2)
             if is_unit(s + 1):
+                open_e(s + 1)
                 for tiles in BANKS:
                     for i in tiles:
                         exp_tile(s + 1, i)
@@ -340,32 +399,43 @@ def tile_tatt_pa_t_kernel(tc, x, tem_embedding, Wv, bv, q, k, out):
                 scale_scores(s + 2, 0)
             if is_unit(s + 3):
                 fill_scores(s + 3, 0)
-            if is_unit(s - 2):
-                normalise(s - 2)
+            if is_unit(s - 3):
+                normalise(s - 3)
             if is_unit(s - 1):
                 quantise_e(s - 1)
-                attend(s - 1)
-            if is_unit(s - 3):
-                store(s - 3)
+                if s % 2 == 0:
+                    quantise_pair((s - 1) // 2)
             if is_unit(s - 2):
-                transpose_out(s - 2)
+                attend(s - 2)
+            if is_unit(s - 4):
+                store(s - 4)
+            if is_unit(s - 3):
+                transpose_out(s - 3)
             if is_unit(s + 2):
                 scale_scores(s + 2, 1)
             if is_unit(s + 3):
                 fill_scores(s + 3, 1)
             if is_unit(s + 1):
                 add_bias(s + 1)
-            if is_unit(s + 2):
+            if s > -2 and is_unit(s + 2):
                 project_v(s + 2)
             if is_unit(s):
-                regroup_e(s, 0)
-                regroup_e(s, 1)
+                regroup_e(s)
+                if s % 2 == 1:
+                    regroup_pair(s // 2)
             if is_unit(s + 2):
                 scale_scores(s + 2, 2)
             if is_unit(s + 3):
                 fill_scores(s + 3, 2)
             if is_unit(s + 1):
                 quantise_v(s + 1)
+                if s % 2 == 0:
+                    spread_v((s + 1) // 2)
                 nc.vector.reciprocal(live[("inv", s + 1)][:], live[("sum", s + 1)][:])
-            if is_unit(s + 5) and (s + 5) % HEADS == 0:
-                quantise_x((s + 5) // HEADS)
+            if s == -3:
+                regroup_w()
+            if s == -2:
+                prepare_projection()
+                project_v(0)
+            if s > 0 and is_unit(s + 3) and (s + 3) % HEADS == 0:
+                quantise_x((s + 3) // HEADS)

@@ -79,14 +79,16 @@ def tile_tatt_pa_t_kernel(tc, x, tem_embedding, Wv, bv, q, k, out):
         k_0 = k[0, :, 0, :].rearrange("(h c) t -> c h t", c=P)
         nc.sync.dma_start(out=q_g[:, 0:1, :], in_=q_0[:, 0:1, :])
         nc.sync.dma_start(out=k_g[:, 0:1, :], in_=k_0[:, 0:1, :])
+        nc.sync.dma_start(out=q_g[:, 1:2, :], in_=q_0[:, 1:2, :])
+        nc.sync.dma_start(out=k_g[:, 1:2, :], in_=k_0[:, 1:2, :])
         nc.sync.dma_start(out=wv_sb[:], in_=Wv.rearrange("(a o) c -> o a c", o=P))
         nc.sync.dma_start(out=x_g[:, 0:2, :], in_=x[0, :, 0, :].rearrange("(j p) t -> p j t", p=P))
         nc.sync.dma_start(
             out=x_g[:, 2:4, :], in_=tem_embedding[0, :, 0, :].rearrange("(j p) t -> p j t", p=P)
         )
-        nc.sync.dma_start(out=q_g[:, 1:HEADS, :], in_=q_0[:, 1:HEADS, :])
-        nc.sync.dma_start(out=k_g[:, 1:HEADS, :], in_=k_0[:, 1:HEADS, :])
         nc.sync.dma_start(out=bias_bf[:], in_=bv.partition_broadcast(P))
+        nc.sync.dma_start(out=q_g[:, 2:HEADS, :], in_=q_0[:, 2:HEADS, :])
+        nc.sync.dma_start(out=k_g[:, 2:HEADS, :], in_=k_0[:, 2:HEADS, :])
         live[("q", 0)] = q_g
         live[("k", 0)] = k_g
         live[("x", 0)] = x_g
@@ -190,6 +192,10 @@ def tile_tatt_pa_t_kernel(tc, x, tem_embedding, Wv, bv, q, k, out):
                 accum_out=live[("sum", u)][:, i : i + 1],
             )
 
+        def exp_bank(u, bank):
+            for i in BANKS[bank]:
+                exp_tile(u, i)
+
         def transpose_words(eT_ps, e_tile):
             for g in range(2):
                 nc.tensor.transpose(eT_ps[:, g, :], e_tile[:, g, :].bitcast(F32), ident_f32[:])
@@ -200,16 +206,30 @@ def tile_tatt_pa_t_kernel(tc, x, tem_embedding, Wv, bv, q, k, out):
                 transpose_words(eT_ps[:, block], live[("e", u)][:, block])
             live[("eT", u)] = eT_ps
 
+        def transpose_block(u, block, tag):
+            eT_ps = psum.tile([P, 2, P], F32, name="eT_block", tag=tag)
+            transpose_words(eT_ps, live[("e", u)][:, block])
+            live[("eT", u, block)] = eT_ps
+
         def transpose_pair(m):
             eT_ps = psum.tile([P, 2, P], F32, name="eT_pair", tag="eT_pair")
             transpose_words(eT_ps, live[("e_pair", m)])
             live[("eT_pair", m)] = eT_ps
 
-        def regroup_e(u):
+        def open_grouped(u):
             live[("eg", u)] = work.tile([P, 2 * P * PACK], BF16, name="e_grouped", align_bytes=64)
+
+        def regroup_e(u):
+            open_grouped(u)
             nc.scalar.copy(
                 out=live[("eg", u)][:].bitcast(F32).rearrange("p (k t g) -> p k t g", k=2, g=2),
                 in_=live[("eT", u)][:].rearrange("p k g t -> p k t g"),
+            )
+
+        def regroup_block(copy, u, block):
+            copy(
+                out=live[("eg", u)][:].bitcast(F32).rearrange("p (k t g) -> p k t g", k=2, g=2)[:, block],
+                in_=live[("eT", u, block)][:].rearrange("p g t -> p t g"),
             )
 
         def regroup_pair(m):
@@ -227,6 +247,18 @@ def tile_tatt_pa_t_kernel(tc, x, tem_embedding, Wv, bv, q, k, out):
             )
             live[("ec", u)] = (e_codes, e_scales)
 
+        def quantise_block(u, block):
+            if ("ec", u) not in live:
+                e_codes = work.tile([P, 2 * P], U32, name="e_codes", align_bytes=64, bufs=3)
+                e_scales = work.tile([P, 2 * P], U8, name="e_scales", align_bytes=64, bufs=3)
+                live[("ec", u)] = (e_codes, e_scales)
+            e_codes, e_scales = live[("ec", u)]
+            nc.vector.quantize_mx(
+                out=e_codes[:, block * P : (block + 1) * P].bitcast(FP8X4),
+                scales=e_scales[:, block * P : (block + 1) * P],
+                in_=live[("eg", u)][:, block * P * PACK : (block + 1) * P * PACK],
+            )
+
         def quantise_pair(m):
             p_codes = work.tile([P, P], U32, name="p_codes", align_bytes=64)
             p_scales = work.tile([P, P], U8, name="p_scales", align_bytes=64)
@@ -238,16 +270,22 @@ def tile_tatt_pa_t_kernel(tc, x, tem_embedding, Wv, bv, q, k, out):
         def regroup_x(engine, group, piece):
             if piece == 0:
                 live[("xg", group)] = work.tile([P, T * PACK], BF16, name="x_grouped", align_bytes=64)
-            engine.tensor_scalar(
-                out=live[("xg", group)][:, piece * P * PACK : (piece + 1) * P * PACK].rearrange(
-                    "p (w j) -> p w j", j=PACK
-                ),
-                in0=live[("x", group)][:].rearrange("p j (w s) -> p s w j", s=PACK)[:, piece],
-                scalar1=1.0,
-                scalar2=0.0,
-                op0=ALU.mult,
-                op1=ALU.add,
+            parts = 4 if engine is nc.gpsimd else 1
+            width = P // parts
+            source = live[("x", group)][:].rearrange("p j (w s) -> p s w j", s=PACK)[:, piece]
+            target = live[("xg", group)][:, piece * P * PACK : (piece + 1) * P * PACK].rearrange(
+                "p (w j) -> p w j", j=PACK
             )
+            for part in range(parts):
+                rows = slice(part * width, (part + 1) * width)
+                engine.tensor_scalar(
+                    out=target[:, rows],
+                    in0=source[:, rows],
+                    scalar1=1.0,
+                    scalar2=0.0,
+                    op0=ALU.mult,
+                    op1=ALU.add,
+                )
 
         def quantise_x(group):
             x_codes = work.tile([P, T], U32, name="x_codes", align_bytes=64)
@@ -301,21 +339,23 @@ def tile_tatt_pa_t_kernel(tc, x, tem_embedding, Wv, bv, q, k, out):
                 rows = slice(64 * odd, 64 * odd + 64)
                 nc.sync.dma_start(out=v_p[rows, odd, FOR_TILE_1, :], in_=v_f[0:64, odd, :])
 
-        def attend(u):
+        def attend(u, tiles=(3, 2, 0, 1), tag="oT"):
             ring, odd = u // 2 % V_RING, u % 2
             v_p = v_part[ring]
-            main = live[("ec", u)]
-            oT_ps = psum.tile([P, TILES, DH], F32, name="oT_ps", tag="oT")
-            for i, e_tile, block, v_words in (
-                (3, main, 0, v_full[ring][:, odd, :]),
-                (2, main, 1, v_p[:, odd, FOR_TILE_2, :]),
-                (0, main, 1, v_p[:, odd, FOR_TILE_0, :]),
-                (1, live[("pc", u // 2)], 0, v_p[:, odd, FOR_TILE_1, :]),
-            ):
-                e_codes, e_scales = e_tile
+            main, pair = live[("ec", u)], live[("pc", u // 2)]
+            operands = (
+                (main, 1, v_p[:, odd, FOR_TILE_0, :]),
+                (pair, 0, v_p[:, odd, FOR_TILE_1, :]),
+                (main, 1, v_p[:, odd, FOR_TILE_2, :]),
+                (main, 0, v_full[ring][:, odd, :]),
+            )
+            lowest = min(tiles)
+            oT_ps = psum.tile([P, len(tiles), DH], F32, name="oT_ps", tag=tag)
+            for i in tiles:
+                (e_codes, e_scales), block, v_words = operands[i]
                 v_codes, v_scales = mx_operand(v_words)
                 nc.tensor.matmul_mx(
-                    out=oT_ps[:, i, :],
+                    out=oT_ps[:, i - lowest, :],
                     lhsT=e_codes[:, block * P : (block + 1) * P].bitcast(FP8X4),
                     lhsT_scale=e_scales[:, block * P : (block + 1) * P],
                     rhs=v_codes,
@@ -323,38 +363,43 @@ def tile_tatt_pa_t_kernel(tc, x, tem_embedding, Wv, bv, q, k, out):
                     start=True,
                     stop=True,
                 )
-            live[("oT", u)] = oT_ps
+            live[("oT", u, lowest)] = oT_ps
 
-        def normalise(u):
-            o_rows = work.tile([P, TILES, DH], F32, name="o_rows")
-            if u % 2 == 1:
-                for i in range(TILES):
+        def normalise(engine, u, first=0, count=TILES):
+            if ("or", u) not in live:
+                live[("or", u)] = work.tile([P, TILES, DH], F32, name="o_rows")
+            oT_ps, o_rows, inv = live[("oT", u, first)], live[("or", u)], live[("inv", u)]
+            if engine is nc.scalar:
+                for i in range(count):
                     nc.scalar.activation(
-                        out=o_rows[:, i, :],
-                        in_=live[("oT", u)][:, i, :],
+                        out=o_rows[:, first + i, :],
+                        in_=oT_ps[:, i, :],
                         func=ACT.Copy,
-                        scale=live[("inv", u)][:, i : i + 1],
+                        scale=inv[:, first + i : first + i + 1],
                     )
             else:
                 nc.vector.tensor_tensor(
-                    out=o_rows[:],
-                    in0=live[("oT", u)][:],
-                    in1=live[("inv", u)][:].unsqueeze(2).to_broadcast([P, TILES, DH]),
+                    out=o_rows[:, first : first + count, :],
+                    in0=oT_ps[:],
+                    in1=inv[:, first : first + count].unsqueeze(2).to_broadcast([P, count, DH]),
                     op=ALU.mult,
                 )
-            live[("or", u)] = o_rows
 
-        def transpose_out(u):
-            o_ps = psum.tile([P, T], F32, name="o_ps", tag="o")
-            for i in range(TILES):
-                nc.tensor.transpose(o_ps[:, i * P : (i + 1) * P], live[("or", u)][:, i, :], ident_f32[:])
-            live[("o", u)] = o_ps
+        def transpose_out(u, first=0, count=TILES, tag="o"):
+            o_ps = psum.tile([P, count * P], F32, name="o_ps", tag=tag)
+            for i in range(count):
+                nc.tensor.transpose(
+                    o_ps[:, i * P : (i + 1) * P], live[("or", u)][:, first + i, :], ident_f32[:]
+                )
+            live[("o", u, first)] = o_ps
 
-        def store(u):
+        def store(copy, u, first=0, count=TILES):
             group, b, n, h = unit_of(u)
-            o_sb = work.tile([P, T], F32, name="o_sb", bufs=4)
-            nc.scalar.copy(out=o_sb[:], in_=live[("o", u)][:])
-            nc.sync.dma_start(out=out[b, h * DH : (h + 1) * DH, n, :], in_=o_sb[:])
+            o_sb = work.tile([P, count * P], F32, name="o_sb", bufs=6)
+            copy(out=o_sb[:], in_=live[("o", u, first)][:])
+            nc.sync.dma_start(
+                out=out[b, h * DH : (h + 1) * DH, n, first * P : (first + count) * P], in_=o_sb[:]
+            )
 
         def regroup_w():
             for pair in range(2):
@@ -364,8 +409,7 @@ def tile_tatt_pa_t_kernel(tc, x, tem_embedding, Wv, bv, q, k, out):
                         nc.tensor.transpose(
                             wT_ps[:, a, j, :], wv_sb[:, 2 * pair + a, j * P : (j + 1) * P], ident_bf[:]
                         )
-                copy = nc.scalar.copy if pair == 0 else nc.vector.tensor_copy
-                copy(
+                nc.scalar.copy(
                     out=w_grouped[:, pair * 2 * P * PACK : (pair + 1) * 2 * P * PACK].rearrange(
                         "p (a o j) -> p a o j", a=2, j=PACK
                     ),
@@ -375,32 +419,55 @@ def tile_tatt_pa_t_kernel(tc, x, tem_embedding, Wv, bv, q, k, out):
         def prepare_projection():
             for piece in range(PACK):
                 regroup_x(nc.vector if piece < 2 else nc.gpsimd, 0, piece)
-            for piece in range(2):
+            for piece in range(3):
                 regroup_x(nc.gpsimd, 1, piece)
             nc.vector.quantize_mx(out=w_codes[:].bitcast(FP8X4), scales=w_scales[:], in_=w_grouped[:])
             quantise_x(0)
 
-        for s in range(-3, UNITS + 4):
-            if s >= 0 and s % HEADS == 0 and s // HEADS + LOADS_AHEAD < GROUPS:
+
+        banks = range(len(BANKS))
+        for bank in banks:
+            fill_scores(0, bank)
+        open_unit(0)
+        open_e(0)
+        for bank in banks:
+            scale_scores(0, bank)
+            fill_scores(1, bank)
+            exp_bank(0, bank)
+        regroup_w()
+        open_unit(1)
+        for bank in banks:
+            scale_scores(1, bank)
+            fill_scores(2, bank)
+        nc.vector.reciprocal(live[("inv", 0)][:], live[("sum", 0)][:])
+        transpose_e(0)
+        prepare_projection()
+        project_v(0)
+        add_bias(0)
+        project_v(1)
+        quantise_v(0)
+
+        last = UNITS - 1
+        for s in range(last):
+            if s % HEADS == 1 and s // HEADS + LOADS_AHEAD < GROUPS:
                 load_group(s // HEADS + LOADS_AHEAD)
-            if s >= -1 and is_unit(s + 7):
+            if is_unit(s + 7):
                 regroup_x(nc.gpsimd, (s + 7) // HEADS, (s + 7) % HEADS)
-            if is_unit(s):
+            if s > 0:
                 transpose_e(s)
-                if s % 2 == 1:
-                    transpose_pair(s // 2)
-            if is_unit(s + 1):
-                open_e(s + 1)
-                for tiles in BANKS:
-                    for i in tiles:
-                        exp_tile(s + 1, i)
+            if s % 2 == 1:
+                transpose_pair(s // 2)
+            open_e(s + 1)
+            for bank in banks:
+                exp_bank(s + 1, bank)
             if is_unit(s + 2):
                 open_unit(s + 2)
                 scale_scores(s + 2, 0)
             if is_unit(s + 3):
                 fill_scores(s + 3, 0)
+            scalar_free = is_unit(s + 2)
             if is_unit(s - 3):
-                normalise(s - 3)
+                normalise(nc.scalar if s % 2 == 0 and scalar_free else nc.vector, s - 3)
             if is_unit(s - 1):
                 quantise_e(s - 1)
                 if s % 2 == 0:
@@ -408,34 +475,58 @@ def tile_tatt_pa_t_kernel(tc, x, tem_embedding, Wv, bv, q, k, out):
             if is_unit(s - 2):
                 attend(s - 2)
             if is_unit(s - 4):
-                store(s - 4)
+                store(nc.scalar.copy if scalar_free else nc.vector.tensor_copy, s - 4)
             if is_unit(s - 3):
                 transpose_out(s - 3)
             if is_unit(s + 2):
                 scale_scores(s + 2, 1)
             if is_unit(s + 3):
                 fill_scores(s + 3, 1)
-            if is_unit(s + 1):
-                add_bias(s + 1)
-            if s > -2 and is_unit(s + 2):
+            add_bias(s + 1)
+            if is_unit(s + 2):
                 project_v(s + 2)
-            if is_unit(s):
-                regroup_e(s)
-                if s % 2 == 1:
-                    regroup_pair(s // 2)
+            regroup_e(s)
+            if s % 2 == 1:
+                regroup_pair(s // 2)
             if is_unit(s + 2):
                 scale_scores(s + 2, 2)
             if is_unit(s + 3):
                 fill_scores(s + 3, 2)
-            if is_unit(s + 1):
-                quantise_v(s + 1)
-                if s % 2 == 0:
-                    spread_v((s + 1) // 2)
-                nc.vector.reciprocal(live[("inv", s + 1)][:], live[("sum", s + 1)][:])
-            if s == -3:
-                regroup_w()
-            if s == -2:
-                prepare_projection()
-                project_v(0)
-            if s > 0 and is_unit(s + 3) and (s + 3) % HEADS == 0:
+            quantise_v(s + 1)
+            if s % 2 == 0:
+                spread_v((s + 1) // 2)
+            nc.vector.reciprocal(live[("inv", s + 1)][:], live[("sum", s + 1)][:])
+            if is_unit(s + 3) and (s + 3) % HEADS == 0:
                 quantise_x((s + 3) // HEADS)
+
+        transpose_block(last, 1, "s1")
+        transpose_pair(last // 2)
+        transpose_block(last, 0, "s0")
+        normalise(nc.vector, last - 3)
+        store(nc.scalar.copy, last - 4)
+        transpose_out(last - 3)
+        attend(last - 2)
+        open_grouped(last)
+        regroup_block(nc.vector.tensor_copy, last, 1)
+        regroup_block(nc.scalar.copy, last, 0)
+        quantise_e(last - 1)
+        regroup_pair(last // 2)
+        quantise_block(last, 1)
+        quantise_block(last, 0)
+        quantise_pair(last // 2)
+        attend(last - 1, tag="s2")
+        attend(last, tiles=(3, 2), tag="v")
+        attend(last, tiles=(0, 1), tag="eT_main")
+        normalise(nc.vector, last - 2)
+        transpose_out(last - 2, tag="s1")
+        store(nc.scalar.copy, last - 3)
+        normalise(nc.vector, last - 1)
+        transpose_out(last - 1, tag="o")
+        normalise(nc.scalar, last, 0, 2)
+        normalise(nc.vector, last, 2, 2)
+        transpose_out(last, 0, 2, tag="eT_pair")
+        transpose_out(last, 2, 2, tag="s0")
+        store(nc.scalar.copy, last - 2)
+        store(nc.vector.tensor_copy, last - 1)
+        store(nc.scalar.copy, last, 0, 2)
+        store(nc.vector.tensor_copy, last, 2, 2)

@@ -159,9 +159,9 @@ def tile_tatt_pa_t_kernel(tc, x, tem_embedding, Wv, bv, q, k, out):
                 columns = slice(first, first + (i + 1) * P)
                 first += (i + 1) * P
                 nc.vector.tensor_scalar(
-                    out=s_sb[:, columns].rearrange("p (g w r) -> p g w r", g=2, r=2),
+                    out=s_sb[:, columns].rearrange("p (g b x) -> p g b x", g=2, x=P // 2),
                     in0=live[("s_ps", u, bank)][:, columns].rearrange(
-                        "p (w g r) -> p g w r", g=2, r=2
+                        "p (b g x) -> p g b x", g=2, x=P // 2
                     ),
                     scalar1=-SCALE,
                     scalar2=None,
@@ -270,17 +270,16 @@ def tile_tatt_pa_t_kernel(tc, x, tem_embedding, Wv, bv, q, k, out):
         def regroup_x(engine, group, piece):
             if piece == 0:
                 live[("xg", group)] = work.tile([P, T * PACK], BF16, name="x_grouped", align_bytes=64)
-            parts = 4 if engine is nc.gpsimd else 1
-            width = P // parts
-            source = live[("x", group)][:].rearrange("p j (w s) -> p s w j", s=PACK)[:, piece]
+            g, r = divmod(piece, 2)
+            source = live[("x", group)][:].rearrange("p j (b g w r) -> p g r b w j", g=2, w=32, r=2)
             target = live[("xg", group)][:, piece * P * PACK : (piece + 1) * P * PACK].rearrange(
-                "p (w j) -> p w j", j=PACK
+                "p (b w j) -> p b w j", b=TILES, j=PACK
             )
-            for part in range(parts):
-                rows = slice(part * width, (part + 1) * width)
+            width = 1 if engine is nc.gpsimd else TILES
+            for b in range(0, TILES, width):
                 engine.tensor_scalar(
-                    out=target[:, rows],
-                    in0=source[:, rows],
+                    out=target[:, b : b + width],
+                    in0=source[:, g, r, b : b + width],
                     scalar1=1.0,
                     scalar2=0.0,
                     op0=ALU.mult,

@@ -328,15 +328,14 @@ def tile_tatt_pa_t_kernel(tc, x, tem_embedding, Wv, bv, q, k, out):
             codes, scales = mx_operand(v_full[u // 2 % V_RING][:, u % 2, :])
             nc.vector.quantize_mx(out=codes, scales=scales, in_=live[("vg", u)][:])
 
-        def spread_v(m):
-            v_f = v_full[m % V_RING][:].bitcast(I32)
-            v_p = v_part[m % V_RING][:].bitcast(I32)
-            nc.sync.dma_start(out=v_p[0:64, :, FOR_TILE_2, :], in_=v_f[0:64, :, :])
-            nc.sync.dma_start(out=v_p[64:96, :, FOR_TILE_2, :], in_=v_f[64:96, :, :])
-            nc.sync.dma_start(out=v_p[96:128, :, FOR_TILE_0, :], in_=v_f[0:32, :, :])
-            for odd in range(2):
-                rows = slice(64 * odd, 64 * odd + 64)
-                nc.sync.dma_start(out=v_p[rows, odd, FOR_TILE_1, :], in_=v_f[0:64, odd, :])
+        def spread_v(u):
+            m, odd = divmod(u, 2)
+            v_f = v_full[m % V_RING][:, odd, :].bitcast(I32)
+            v_p = v_part[m % V_RING][:, odd].bitcast(I32)
+            nc.sync.dma_start(out=v_p[0:64, FOR_TILE_2, :], in_=v_f[0:64, :])
+            nc.sync.dma_start(out=v_p[64:96, FOR_TILE_2, :], in_=v_f[64:96, :])
+            nc.sync.dma_start(out=v_p[96:128, FOR_TILE_0, :], in_=v_f[0:32, :])
+            nc.sync.dma_start(out=v_p[64 * odd : 64 * odd + 64, FOR_TILE_1, :], in_=v_f[0:64, :])
 
         def attend(u, tiles=(3, 2, 0, 1), tag="oT"):
             ring, odd = u // 2 % V_RING, u % 2
@@ -366,7 +365,7 @@ def tile_tatt_pa_t_kernel(tc, x, tem_embedding, Wv, bv, q, k, out):
 
         def normalise(engine, u, first=0, count=TILES):
             if ("or", u) not in live:
-                live[("or", u)] = work.tile([P, TILES, DH], F32, name="o_rows")
+                live[("or", u)] = work.tile([P, TILES, DH], F32, name="o_rows", bufs=4)
             oT_ps, o_rows, inv = live[("oT", u, first)], live[("or", u)], live[("inv", u)]
             if engine is nc.scalar:
                 for i in range(count):
@@ -445,6 +444,7 @@ def tile_tatt_pa_t_kernel(tc, x, tem_embedding, Wv, bv, q, k, out):
         add_bias(0)
         project_v(1)
         quantise_v(0)
+        spread_v(0)
 
         last = UNITS - 1
         for s in range(last):
@@ -492,8 +492,7 @@ def tile_tatt_pa_t_kernel(tc, x, tem_embedding, Wv, bv, q, k, out):
             if is_unit(s + 3):
                 fill_scores(s + 3, 2)
             quantise_v(s + 1)
-            if s % 2 == 0:
-                spread_v((s + 1) // 2)
+            spread_v(s + 1)
             nc.vector.reciprocal(live[("inv", s + 1)][:], live[("sum", s + 1)][:])
             if is_unit(s + 3) and (s + 3) % HEADS == 0:
                 quantise_x((s + 3) // HEADS)

from contextlib import ExitStack
import math

import concourse.mybir as mybir
from concourse.masks import make_identity

F32 = mybir.dt.float32
BF16 = mybir.dt.bfloat16
U32 = mybir.dt.uint32
U8 = mybir.dt.uint8
I32 = mybir.dt.int32
FP8X4 = mybir.dt.float8_e4m3fn_x4
ALU = mybir.AluOpType
ACT = mybir.ActivationFunctionType
AXIS = mybir.AxisListType

P = 128
PACK = 4
BATCH, NODES, HEADS, T, DH = 2, 4, 4, 512, 128
CIN = 512
TILES = T // P
GROUPS = BATCH * NODES
UNITS = GROUPS * HEADS
V_WORDS = DH + DH // PACK
V_RING = 3
FOR_TILE_2, FOR_TILE_0, FOR_TILE_1 = range(3)
LOADS_AHEAD = 3
SCALE = 1.0 / math.sqrt(DH)
MASKED = -(2.0**30)
BANKS = ((1,), (0, 2), (3,))

FLOPS = 3 * 2 * BATCH * NODES * T * CIN * CIN


def tile_tatt_pa_t_kernel(tc, x, tem_embedding, Wv, bv, q, k, out):
    nc = tc.nc
    with ExitStack() as ctx:
        const = ctx.enter_context(tc.tile_pool(name="const", bufs=1))
        loads = ctx.enter_context(tc.tile_pool(name="loads", bufs=GROUPS))
        work = ctx.enter_context(tc.tile_pool(name="work", bufs=2))
        small = ctx.enter_context(tc.tile_pool(name="small", bufs=6))
        psum = ctx.enter_context(tc.psum_pool(name="psum", bufs=1))
        ctx.enter_context(tc.manual_schedule())

        live = {}

        def unit_of(u):
            group, h = divmod(u, HEADS)
            b, n = divmod(group, NODES)
            return group, b, n, h

        def is_unit(u):
            return 0 <= u < UNITS

        def load_group(group):
            b, n = divmod(group, NODES)
            q_g = loads.tile([P, HEADS, T], BF16, name="q_g")
            k_g = loads.tile([P, HEADS, T], BF16, name="k_g")
            x_g = loads.tile([P, PACK, T], BF16, name="x_g")
            nc.sync.dma_start(
                out=x_g[:, 0:2, :], in_=x[b, :, n, :].rearrange("(j p) t -> p j t", p=P)
            )
            nc.sync.dma_start(
                out=x_g[:, 2:4, :],
                in_=tem_embedding[b, :, n, :].rearrange("(j p) t -> p j t", p=P),
            )
            nc.sync.dma_start(out=q_g[:], in_=q[b, :, n, :].rearrange("(h c) t -> c h t", c=P))
            nc.sync.dma_start(out=k_g[:], in_=k[b, :, n, :].rearrange("(h c) t -> c h t", c=P))
            live[("q", group)] = q_g
            live[("k", group)] = k_g
            live[("x", group)] = x_g

        wv_sb = const.tile([P, PACK, CIN], BF16, name="wv_sb")
        bias_bf = const.tile([P, CIN], BF16, name="bias_bf")
        q_g = loads.tile([P, HEADS, T], BF16, name="q_g")
        k_g = loads.tile([P, HEADS, T], BF16, name="k_g")
        x_g = loads.tile([P, PACK, T], BF16, name="x_g")
        q_0 = q[0, :, 0, :].rearrange("(h c) t -> c h t", c=P)
        k_0 = k[0, :, 0, :].rearrange("(h c) t -> c h t", c=P)
        nc.sync.dma_start(out=q_g[:, 0:1, :], in_=q_0[:, 0:1, :])
        nc.sync.dma_start(out=k_g[:, 0:1, :], in_=k_0[:, 0:1, :])
        nc.sync.dma_start(out=q_g[:, 1:2, :], in_=q_0[:, 1:2, :])
        nc.sync.dma_start(out=k_g[:, 1:2, :], in_=k_0[:, 1:2, :])
        nc.sync.dma_start(out=wv_sb[:], in_=Wv.rearrange("(a o) c -> o a c", o=P))
        nc.sync.dma_start(out=x_g[:, 0:2, :], in_=x[0, :, 0, :].rearrange("(j p) t -> p j t", p=P))
        nc.sync.dma_start(
            out=x_g[:, 2:4, :], in_=tem_embedding[0, :, 0, :].rearrange("(j p) t -> p j t", p=P)
        )
        nc.sync.dma_start(out=bias_bf[:], in_=bv.partition_broadcast(P))
        nc.sync.dma_start(out=q_g[:, 2:HEADS, :], in_=q_0[:, 2:HEADS, :])
        nc.sync.dma_start(out=k_g[:, 2:HEADS, :], in_=k_0[:, 2:HEADS, :])
        live[("q", 0)] = q_g
        live[("k", 0)] = k_g
        live[("x", 0)] = x_g
        for group in range(1, LOADS_AHEAD):
            load_group(group)

        warm = const.tile([P, 2], F32, name="warm")
        nc.vector.memset(warm[:], 0.0)
        nc.scalar.activation(out=warm[:, 1:2], in_=warm[:, 0:1], func=ACT.Exp)
        ident_bf = const.tile([P, P], BF16, name="ident_bf")
        make_identity(nc, ident_bf[:])
        mask_bf = const.tile([P, P], BF16, name="mask_bf")
        nc.gpsimd.memset(mask_bf[:], 0.0)
        nc.gpsimd.affine_select(
            out=mask_bf[:],
            in_=mask_bf[:],
            compare_op=ALU.is_ge,
            fill=MASKED,
            base=0,
            pattern=[[-1, P]],
            channel_multiplier=1,
        )
        ident_f32 = const.tile([P, P], F32, name="ident_f32")
        make_identity(nc, ident_f32[:])
        v_full, v_part = [], []
        for r in range(V_RING):
            v_f = const.tile([P, 2, V_WORDS], U32, name="v_full%d" % r, align_bytes=64)
            nc.vector.memset(v_f[:, :, DH:V_WORDS].bitcast(I32), 0)
            v_full.append(v_f)
            v_p = const.tile([P, 2, 3, V_WORDS], U32, name="v_part%d" % r, align_bytes=64)
            nc.gpsimd.memset(v_p[:].bitcast(I32), 0)
            v_part.append(v_p)

        w_grouped = const.tile([P, CIN * PACK], BF16, name="w_grouped", align_bytes=64)
        w_codes = const.tile([P, CIN], U32, name="w_codes", align_bytes=64)
        w_scales = const.tile([P, CIN], U8, name="w_scales", align_bytes=64)

        def open_unit(u):
            live[("shift", u)] = small.tile([P, TILES], F32, name="shift")
            live[("sum", u)] = small.tile([P, TILES], F32, name="row_sums")
            live[("inv", u)] = small.tile([P, TILES], F32, name="inv_sums")

        def fill_scores(u, bank):
            group, b, n, h = unit_of(u)
            q_h = live[("q", group)][:, h, :]
            k_h = live[("k", group)][:, h, :]
            s_ps = psum.tile([P, T], F32, name="s_ps", tag="s%d" % bank)
            first = 0
            for i in BANKS[bank]:
                region = s_ps[:, first : first + (i + 1) * P]
                first += (i + 1) * P
                q_i = q_h[:, i * P : (i + 1) * P]
                diagonal = region[:, i * P : (i + 1) * P]
                nc.tensor.matmul(diagonal, lhsT=ident_bf[:], rhs=mask_bf[:], start=True, stop=False)
                nc.tensor.matmul(
                    diagonal, lhsT=q_i, rhs=k_h[:, i * P : (i + 1) * P], start=False, stop=True
                )
                if i > 0:
                    nc.tensor.matmul(
                        region[:, 0 : i * P], lhsT=q_i, rhs=k_h[:, 0 : i * P], start=True, stop=True
                    )
            live[("s_ps", u, bank)] = s_ps

        def scale_scores(u, bank):
            s_sb = work.tile([P, T], F32, name="s_sb%d" % bank, bufs=3)
            first = 0
            for i in BANKS[bank]:
                columns = slice(first, first + (i + 1) * P)
                first += (i + 1) * P
                nc.vector.tensor_scalar(
                    out=s_sb[:, columns].rearrange("p (g b x) -> p g b x", g=2, x=P // 2),
                    in0=live[("s_ps", u, bank)][:, columns].rearrange(
                        "p (b g x) -> p g b x", g=2, x=P // 2
                    ),
                    scalar1=-SCALE,
                    scalar2=None,
                    op0=ALU.mult,
                    op1=ALU.min,
                    accum_out=live[("shift", u)][:, i : i + 1],
                )
                live[("s", u, i)] = s_sb[:, columns]

        def open_e(u):
            live[("e", u)] = work.tile([P, 2, 2, 2 * P], BF16, name="e_main", bufs=3)
            if u % 2 == 0:
                live[("e_pair", u // 2)] = work.tile([P, 2, 2 * P], BF16, name="e_pair")

        def exp_tile(u, i):
            if i == 1:
                e_tile, first = live[("e_pair", u // 2)][:], (u % 2) * P
            elif i == 3:
                e_tile, first = live[("e", u)][:, 0], 0
            else:
                e_tile, first = live[("e", u)][:, 1], 0 if i == 2 else 3 * P // 2
            nc.scalar.activation(
                out=e_tile[:, :, first : first + (i + 1) * P // 2],
                in_=live[("s", u, i)].rearrange("p (g x) -> p g x", g=2),
                func=ACT.Exp,
                bias=live[("shift", u)][:, i : i + 1],
                scale=-1.0,
                accum_out=live[("sum", u)][:, i : i + 1],
            )

        def exp_bank(u, bank):
            for i in BANKS[bank]:
                exp_tile(u, i)

        def transpose_words(eT_ps, e_tile):
            for g in range(2):
                nc.tensor.transpose(eT_ps[:, g, :], e_tile[:, g, :].bitcast(F32), ident_f32[:])

        def transpose_e(u):
            eT_ps = psum.tile([P, 2, 2, P], F32, name="eT_main", tag="eT_main")
            for block in range(2):
                transpose_words(eT_ps[:, block], live[("e", u)][:, block])
            live[("eT", u)] = eT_ps

        def transpose_block(u, block, tag):
            eT_ps = psum.tile([P, 2, P], F32, name="eT_block", tag=tag)
            transpose_words(eT_ps, live[("e", u)][:, block])
            live[("eT", u, block)] = eT_ps

        def transpose_pair(m):
            eT_ps = psum.tile([P, 2, P], F32, name="eT_pair", tag="eT_pair")
            transpose_words(eT_ps, live[("e_pair", m)])
            live[("eT_pair", m)] = eT_ps

        def open_grouped(u):
            live[("eg", u)] = work.tile([P, 2 * P * PACK], BF16, name="e_grouped", align_bytes=64)

        def regroup_e(u):
            open_grouped(u)
            nc.scalar.copy(
                out=live[("eg", u)][:].bitcast(F32).rearrange("p (k t g) -> p k t g", k=2, g=2),
                in_=live[("eT", u)][:].rearrange("p k g t -> p k t g"),
            )

        def regroup_block(copy, u, block):
            copy(
                out=live[("eg", u)][:].bitcast(F32).rearrange("p (k t g) -> p k t g", k=2, g=2)[:, block],
                in_=live[("eT", u, block)][:].rearrange("p g t -> p t g"),
            )

        def regroup_pair(m):
            live[("eg_pair", m)] = work.tile([P, P * PACK], BF16, name="e_grouped_pair", align_bytes=64)
            nc.scalar.copy(
                out=live[("eg_pair", m)][:].bitcast(F32).rearrange("p (t g) -> p t g", g=2),
                in_=live[("eT_pair", m)][:].rearrange("p g t -> p t g"),
            )

        def quantise_e(u):
            e_codes = work.tile([P, 2 * P], U32, name="e_codes", align_bytes=64, bufs=3)
            e_scales = work.tile([P, 2 * P], U8, name="e_scales", align_bytes=64, bufs=3)
            nc.vector.quantize_mx(
                out=e_codes[:].bitcast(FP8X4), scales=e_scales[:], in_=live[("eg", u)][:]
            )
            live[("ec", u)] = (e_codes, e_scales)

        def quantise_block(u, block):
            if ("ec", u) not in live:
                e_codes = work.tile([P, 2 * P], U32, name="e_codes", align_bytes=64, bufs=3)
                e_scales = work.tile([P, 2 * P], U8, name="e_scales", align_bytes=64, bufs=3)
                live[("ec", u)] = (e_codes, e_scales)
            e_codes, e_scales = live[("ec", u)]
            nc.vector.quantize_mx(
                out=e_codes[:, block * P : (block + 1) * P].bitcast(FP8X4),
                scales=e_scales[:, block * P : (block + 1) * P],
                in_=live[("eg", u)][:, block * P * PACK : (block + 1) * P * PACK],
            )

        def quantise_pair(m):
            p_codes = work.tile([P, P], U32, name="p_codes", align_bytes=64)
            p_scales = work.tile([P, P], U8, name="p_scales", align_bytes=64)
            nc.vector.quantize_mx(
                out=p_codes[:].bitcast(FP8X4), scales=p_scales[:], in_=live[("eg_pair", m)][:]
            )
            live[("pc", m)] = (p_codes, p_scales)

        def regroup_x(engine, group, piece):
            if piece == 0:
                live[("xg", group)] = work.tile([P, T * PACK], BF16, name="x_grouped", align_bytes=64)
            g, r = divmod(piece, 2)
            source = live[("x", group)][:].rearrange("p j (b g w r) -> p g r b w j", g=2, w=32, r=2)
            target = live[("xg", group)][:, piece * P * PACK : (piece + 1) * P * PACK].rearrange(
                "p (b w j) -> p b w j", b=TILES, j=PACK
            )
            width = 1 if engine is nc.gpsimd else TILES
            for b in range(0, TILES, width):
                engine.tensor_scalar(
                    out=target[:, b : b + width],
                    in0=source[:, g, r, b : b + width],
                    scalar1=1.0,
                    scalar2=0.0,
                    op0=ALU.mult,
                    op1=ALU.add,
                )

        def quantise_x(group):
            x_codes = work.tile([P, T], U32, name="x_codes", align_bytes=64)
            x_scales = work.tile([P, T], U8, name="x_scales", align_bytes=64)
            nc.vector.quantize_mx(
                out=x_codes[:].bitcast(FP8X4), scales=x_scales[:], in_=live[("xg", group)][:]
            )
            live[("xc", group)] = (x_codes, x_scales)

        def project_v(u):
            group, b, n, h = unit_of(u)
            x_codes, x_scales = live[("xc", group)]
            v_ps = psum.tile([P, PACK, DH], F32, name="v_ps", tag="v")
            for s in range(PACK):
                nc.tensor.matmul_mx(
                    out=v_ps[:, s, :],
                    lhsT=x_codes[:, s * P : (s + 1) * P].bitcast(FP8X4),
                    lhsT_scale=x_scales[:, s * P : (s + 1) * P],
                    rhs=w_codes[:, h * DH : (h + 1) * DH].bitcast(FP8X4),
                    rhs_scale=w_scales[:, h * DH : (h + 1) * DH],
                    start=True,
                    stop=True,
                )
            live[("v_ps", u)] = v_ps

        def add_bias(u):
            group, b, n, h = unit_of(u)
            v_grouped = work.tile([P, DH * PACK], BF16, name="v_grouped", align_bytes=64)
            nc.vector.tensor_tensor(
                out=v_grouped[:].rearrange("p (c s) -> p c s", s=PACK),
                in0=live[("v_ps", u)][:].rearrange("p s c -> p c s"),
                in1=bias_bf[:, h * DH : (h + 1) * DH].unsqueeze(2).to_broadcast([P, DH, PACK]),
                op=ALU.add,
            )
            live[("vg", u)] = v_grouped

        def mx_operand(words):
            return words[:, 0:DH].bitcast(FP8X4), words[:, DH:V_WORDS].bitcast(U8)

        def quantise_v(u):
            codes, scales = mx_operand(v_full[u // 2 % V_RING][:, u % 2, :])
            nc.vector.quantize_mx(out=codes, scales=scales, in_=live[("vg", u)][:])

        def spread_v(u):
            m, odd = divmod(u, 2)
            v_f = v_full[m % V_RING][:, odd, :].bitcast(I32)
            v_p = v_part[m % V_RING][:, odd].bitcast(I32)
            nc.sync.dma_start(out=v_p[0:64, FOR_TILE_2, :], in_=v_f[0:64, :])
            nc.sync.dma_start(out=v_p[64:96, FOR_TILE_2, :], in_=v_f[64:96, :])
            nc.sync.dma_start(out=v_p[96:128, FOR_TILE_0, :], in_=v_f[0:32, :])
            nc.sync.dma_start(out=v_p[64 * odd : 64 * odd + 64, FOR_TILE_1, :], in_=v_f[0:64, :])

        def attend(u, tiles=(3, 2, 0, 1), tag="oT"):
            ring, odd = u // 2 % V_RING, u % 2
            v_p = v_part[ring]
            main, pair = live[("ec", u)], live[("pc", u // 2)]
            operands = (
                (main, 1, v_p[:, odd, FOR_TILE_0, :]),
                (pair, 0, v_p[:, odd, FOR_TILE_1, :]),
                (main, 1, v_p[:, odd, FOR_TILE_2, :]),
                (main, 0, v_full[ring][:, odd, :]),
            )
            lowest = min(tiles)
            oT_ps = psum.tile([P, len(tiles), DH], F32, name="oT_ps", tag=tag)
            for i in tiles:
                (e_codes, e_scales), block, v_words = operands[i]
                v_codes, v_scales = mx_operand(v_words)
                nc.tensor.matmul_mx(
                    out=oT_ps[:, i - lowest, :],
                    lhsT=e_codes[:, block * P : (block + 1) * P].bitcast(FP8X4),
                    lhsT_scale=e_scales[:, block * P : (block + 1) * P],
                    rhs=v_codes,
                    rhs_scale=v_scales,
                    start=True,
                    stop=True,
                )
            live[("oT", u, lowest)] = oT_ps

        def normalise(engine, u, first=0, count=TILES):
            if ("or", u) not in live:
                live[("or", u)] = work.tile([P, TILES, DH], F32, name="o_rows", bufs=4)
            oT_ps, o_rows, inv = live[("oT", u, first)], live[("or", u)], live[("inv", u)]
            if engine is nc.scalar:
                for i in range(count):
                    nc.scalar.activation(
                        out=o_rows[:, first + i, :],
                        in_=oT_ps[:, i, :],
                        func=ACT.Copy,
                        scale=inv[:, first + i : first + i + 1],
                    )
            else:
                nc.vector.tensor_tensor(
                    out=o_rows[:, first : first + count, :],
                    in0=oT_ps[:],
                    in1=inv[:, first : first + count].unsqueeze(2).to_broadcast([P, count, DH]),
                    op=ALU.mult,
                )

        def transpose_out(u, first=0, count=TILES, tag="o"):
            o_ps = psum.tile([P, count * P], F32, name="o_ps", tag=tag)
            for i in range(count):
                nc.tensor.transpose(
                    o_ps[:, i * P : (i + 1) * P], live[("or", u)][:, first + i, :], ident_f32[:]
                )
            live[("o", u, first)] = o_ps

        def store(copy, u, first=0, count=TILES):
            group, b, n, h = unit_of(u)
            o_sb = work.tile([P, count * P], F32, name="o_sb", bufs=6)
            copy(out=o_sb[:], in_=live[("o", u, first)][:])
            nc.sync.dma_start(
                out=out[b, h * DH : (h + 1) * DH, n, first * P : (first + count) * P], in_=o_sb[:]
            )

        def regroup_w():
            for pair in range(2):
                wT_ps = psum.tile([P, 2, PACK, P], BF16, name="wT_ps", tag="oT" if pair == 0 else "o")
                for a in range(2):
                    for j in range(PACK):
                        nc.tensor.transpose(
                            wT_ps[:, a, j, :], wv_sb[:, 2 * pair + a, j * P : (j + 1) * P], ident_bf[:]
                        )
                nc.scalar.copy(
                    out=w_grouped[:, pair * 2 * P * PACK : (pair + 1) * 2 * P * PACK].rearrange(
                        "p (a o j) -> p a o j", a=2, j=PACK
                    ),
                    in_=wT_ps[:].rearrange("p a j o -> p a o j"),
                )

        def prepare_projection():
            for piece in range(PACK):
                regroup_x(nc.vector if piece < 2 else nc.gpsimd, 0, piece)
            for piece in range(3):
                regroup_x(nc.gpsimd, 1, piece)
            nc.vector.quantize_mx(out=w_codes[:].bitcast(FP8X4), scales=w_scales[:], in_=w_grouped[:])
            quantise_x(0)


        banks = range(len(BANKS))
        for bank in banks:
            fill_scores(0, bank)
        open_unit(0)
        open_e(0)
        for bank in banks:
            scale_scores(0, bank)
            fill_scores(1, bank)
            exp_bank(0, bank)
        regroup_w()
        open_unit(1)
        for bank in banks:
            scale_scores(1, bank)
            fill_scores(2, bank)
        nc.vector.reciprocal(live[("inv", 0)][:], live[("sum", 0)][:])
        transpose_e(0)
        prepare_projection()
        project_v(0)
        add_bias(0)
        project_v(1)
        quantise_v(0)
        spread_v(0)

        last = UNITS - 1
        for s in range(last):
            if s % HEADS == 1 and s // HEADS + LOADS_AHEAD < GROUPS:
                load_group(s // HEADS + LOADS_AHEAD)
            if is_unit(s + 7):
                regroup_x(nc.gpsimd, (s + 7) // HEADS, (s + 7) % HEADS)
            if s > 0:
                transpose_e(s)
            if s % 2 == 1:
                transpose_pair(s // 2)
            open_e(s + 1)
            for bank in banks:
                exp_bank(s + 1, bank)
            if is_unit(s + 2):
                open_unit(s + 2)
                scale_scores(s + 2, 0)
            if is_unit(s + 3):
                fill_scores(s + 3, 0)
            scalar_free = is_unit(s + 2)
            if is_unit(s - 3):
                normalise(nc.scalar if s % 2 == 0 and scalar_free else nc.vector, s - 3)
            if is_unit(s - 1):
                quantise_e(s - 1)
                if s % 2 == 0:
                    quantise_pair((s - 1) // 2)
            if is_unit(s - 2):
                attend(s - 2)
            if is_unit(s - 4):
                store(nc.scalar.copy if scalar_free else nc.vector.tensor_copy, s - 4)
            if is_unit(s - 3):
                transpose_out(s - 3)
            if is_unit(s + 2):
                scale_scores(s + 2, 1)
            if is_unit(s + 3):
                fill_scores(s + 3, 1)
            add_bias(s + 1)
            if is_unit(s + 2):
                project_v(s + 2)
            regroup_e(s)
            if s % 2 == 1:
                regroup_pair(s // 2)
            if is_unit(s + 2):
                scale_scores(s + 2, 2)
            if is_unit(s + 3):
                fill_scores(s + 3, 2)
            quantise_v(s + 1)
            spread_v(s + 1)
            nc.vector.reciprocal(live[("inv", s + 1)][:], live[("sum", s + 1)][:])
            if is_unit(s + 3) and (s + 3) % HEADS == 0:
                quantise_x((s + 3) // HEADS)

        transpose_block(last, 1, "s1")
        transpose_pair(last // 2)
        transpose_block(last, 0, "s0")
        normalise(nc.vector, last - 3)
        store(nc.scalar.copy, last - 4)
        transpose_out(last - 3)
        attend(last - 2)
        open_grouped(last)
        regroup_block(nc.vector.tensor_copy, last, 1)
        regroup_block(nc.scalar.copy, last, 0)
        quantise_e(last - 1)
        regroup_pair(last // 2)
        quantise_block(last, 1)
        quantise_block(last, 0)
        quantise_pair(last // 2)
        attend(last - 1, tag="s2")
        attend(last, tiles=(3, 2), tag="v")
        attend(last, tiles=(0, 1), tag="eT_main")
        normalise(nc.vector, last - 2)
        transpose_out(last - 2, tag="s1")
        store(nc.scalar.copy, last - 3)
        normalise(nc.vector, last - 1)
        transpose_out(last - 1, tag="o")
        normalise(nc.scalar, last, 0, 2)
        normalise(nc.vector, last, 2, 2)
        transpose_out(last, 0, 2, tag="eT_pair")
        transpose_out(last, 2, 2, tag="s0")
        store(nc.scalar.copy, last - 2)
        store(nc.vector.tensor_copy, last - 1)
        store(nc.scalar.copy, last, 0, 2)
        store(nc.vector.tensor_copy, last, 2, 2)
